import numpy as np
import ml_dtypes


def mxq(x, axis, fmt="e4m3"):
    dtype, down = {"e4m3": (ml_dtypes.float8_e4m3fn, 7), "e5m2": (ml_dtypes.float8_e5m2, 14)}[fmt]
    v = np.moveaxis(np.asarray(x, np.float32).astype(ml_dtypes.bfloat16).astype(np.float64), axis, -1)
    blocks = v.reshape(v.shape[:-1] + (-1, 32))
    amax = np.abs(blocks).max(-1, keepdims=True)
    byte = np.maximum(np.where(amax > 0, np.frexp(amax)[1] - 1 + 127, 0) - down, 1)
    scale = np.exp2(byte - 127.0)
    codes = (blocks / scale).astype(np.float32).astype(dtype).astype(np.float64)
    return np.moveaxis((codes * scale).reshape(v.shape), -1, axis)


WIDE = False


def mx_kscale(k):
    if not WIDE:
        return np.ones(k)
    levels = np.array([10, -10, 5, -5, 0])
    if k % 512:
        return np.exp2(np.random.permutation(np.resize(levels, k // 32))).repeat(32)
    a = np.empty((k // 512, 16))
    for p in range(k // 512):
        a[p, :8] = np.random.permutation(np.resize(levels, 8))
        for g in range(8):
            far = levels[np.abs(levels - a[p, g]) >= 10]
            a[p, g + 8] = far[np.random.randint(len(far))]
    return np.exp2(a.ravel()).repeat(32)


BF16 = ml_dtypes.bfloat16


def bf(x):
    return np.asarray(x, np.float32).astype(BF16)


def f64(x):
    return np.asarray(x).astype(np.float64)


B, L, D, H, DH = 4, 256, 1024, 16, 64
THETA = 100000.0
E = H * DH


def rope(t):
    pos = np.arange(L, dtype=np.float64)
    inv_freq = 1.0 / THETA ** (np.arange(0, DH, 2, dtype=np.float64) / DH)
    ang = pos[:, None] * inv_freq[None, :]
    cos = np.cos(ang)[:, :, None]
    sin = np.sin(ang)[:, :, None]
    tp = t.reshape(*t.shape[:-1], DH // 2, 2)
    x1, x2 = tp[..., 0], tp[..., 1]
    rot = np.stack([-x2, x1], axis=-1)
    out = tp * cos + rot * sin
    return out.reshape(*t.shape)


def setup_inputs():
    s = mx_kscale(D)
    return {"x": bf(np.random.standard_normal((B, L, D)) * s),
            "W": bf(np.random.standard_normal((3 * E, D)) / np.sqrt(D) / s)}


def reference(x, W):
    qkv = mxq(f64(x), 2, "e4m3") @ mxq(f64(W), 1, "e4m3").T
    qkv = qkv.reshape(B, L, 3, H, DH)
    qkv = np.transpose(qkv, (0, 3, 1, 2, 4))
    q, k, v = qkv[..., 0, :], qkv[..., 1, :], qkv[..., 2, :]
    return rope(q), rope(k), np.ascontiguousarray(v)

@@ -1,0 +1,265 @@
+from contextlib import ExitStack
+import math
+
+import concourse.mybir as mybir
+from concourse.masks import make_identity
+
+F32 = mybir.dt.float32
+BF16 = mybir.dt.bfloat16
+I32 = mybir.dt.int32
+U32 = mybir.dt.uint32
+U8 = mybir.dt.uint8
+FP8X4 = mybir.dt.float8_e4m3fn_x4
+ALU = mybir.AluOpType
+ACT = mybir.ActivationFunctionType
+
+B, L, D, H, DH = 4, 256, 1024, 16, 64
+THETA = 100000.0
+FLOPS = 2 * B * L * D * 3 * H * DH
+
+P = 128
+PACK = 4
+PASSES = D // (P * PACK)
+WORDS = D // 2
+CHUNKS = WORDS // P
+J = B * L // P
+B_BITS, J_BITS = 2, 3
+assert (1 << B_BITS, 1 << J_BITS) == (B, J)
+N_TILE = 512
+PAIRS = DH // 2
+HEADS = N_TILE // DH
+QUERY, KEY, VALUE = 0, 1, 2
+
+ROUND = 1.5 * 2.0**23
+TURN_HI = 6.28125
+TURN_LO = 2.0 * math.pi - TURN_HI
+
+
+def build_rotation_table(nc, pool):
+    partition = pool.tile([P, 1], I32)
+    nc.gpsimd.iota(partition[:], pattern=[[0, 1]], base=0, channel_multiplier=1)
+    token = pool.tile([P, J], I32)
+    nc.gpsimd.iota(token[:], pattern=[[1, J]], base=0, channel_multiplier=0)
+    first_int = pool.tile([P, 1], I32)
+    nc.vector.tensor_scalar(
+        out=first_int[:],
+        in0=partition[:],
+        scalar1=B_BITS,
+        scalar2=J_BITS,
+        op0=ALU.logical_shift_right,
+        op1=ALU.logical_shift_left,
+    )
+    first = pool.tile([P, 1], F32)
+    nc.vector.tensor_copy(out=first[:], in_=first_int[:])
+    position = pool.tile([P, J], F32)
+    nc.vector.tensor_copy(out=position[:], in_=token[:])
+    nc.vector.tensor_scalar_add(out=position[:], in0=position[:], scalar1=first[:, 0:1])
+
+    frequency = pool.tile([P, PAIRS], F32)
+    nc.vector.memset(frequency[:, 0:1], 1.0)
+    have = 1
+    while have < PAIRS:
+        nc.vector.tensor_scalar_mul(
+            out=frequency[:, have : 2 * have],
+            in0=frequency[:, 0:have],
+            scalar1=THETA ** (-2.0 * have / DH),
+        )
+        have *= 2
+
+    angle = pool.tile([P, J, PAIRS], F32)
+    nc.vector.tensor_tensor(
+        out=angle[:],
+        in0=position[:].unsqueeze(2).to_broadcast([P, J, PAIRS]),
+        in1=frequency[:].unsqueeze(1).to_broadcast([P, J, PAIRS]),
+        op=ALU.mult,
+    )
+
+    turns = pool.tile([P, J, PAIRS], F32)
+    nc.vector.tensor_scalar(
+        out=turns[:], in0=angle[:], scalar1=0.5 / math.pi, scalar2=ROUND, op0=ALU.mult, op1=ALU.add
+    )
+    nc.vector.tensor_scalar_add(out=turns[:], in0=turns[:], scalar1=-ROUND)
+    for part_of_turn in (TURN_HI, TURN_LO):
+        nc.vector.scalar_tensor_tensor(
+            out=angle[:], in0=turns[:], scalar=-part_of_turn, in1=angle[:], op0=ALU.mult, op1=ALU.add
+        )
+
+    phase_int = pool.tile([P, 2, 2], I32)
+    nc.gpsimd.iota(phase_int[:], pattern=[[1, 2], [-1, 2]], base=0, channel_multiplier=0)
+    phase = pool.tile([P, 2, 2], F32)
+    nc.vector.tensor_scalar_mul(out=phase[:], in0=phase_int[:], scalar1=0.5 * math.pi)
+
+    table = pool.tile([P, J, 2, PAIRS, 2], F32)
+    for source in range(2):
+        nc.vector.tensor_tensor(
+            out=table[:, :, source],
+            in0=angle[:].unsqueeze(3).to_broadcast([P, J, PAIRS, 2]),
+            in1=phase[:, source].unsqueeze(1).unsqueeze(1).to_broadcast([P, J, PAIRS, 2]),
+            op=ALU.add,
+        )
+    nc.scalar.activation(out=table[:], in_=table[:], func=ACT.Sin, scale=0.5)
+    nc.vector.tensor_tensor(out=table[:], in0=table[:], in1=table[:], op=ALU.mult)
+    nc.vector.tensor_scalar(
+        out=table[:], in0=table[:], scalar1=-2.0, scalar2=1.0, op0=ALU.mult, op1=ALU.add
+    )
+    return table
+
+
+def quantise_rows(nc, pools, identity, blocks, codes, scales):
+    columns = P * len(blocks)
+    grouped = pools["grouped"].tile(
+        [P, PASSES, columns, PACK], BF16, align_bytes=64, tag="grouped%d" % columns
+    )
+    grouped_words = grouped[:].bitcast(F32)
+    for block, words in enumerate(blocks):
+        flipped = pools["flipped"].tile([P, CHUNKS, P], F32)
+        for s in range(PASSES):
+            for u in range(2):
+                nc.tensor.transpose(
+                    flipped[:, 2 * s + u, :],
+                    words[:, 2 * P * s + u : 2 * P * (s + 1) : 2],
+                    identity[:],
+                )
+        nc.scalar.copy(
+            out=grouped_words[:, :, block * P : (block + 1) * P, :],
+            in_=flipped[:].rearrange("p (s u) r -> p s r u", u=2),
+        )
+    nc.vector.quantize_mx(
+        out=codes.rearrange("p s n -> p (s n)").bitcast(FP8X4),
+        scales=scales.rearrange("p s n -> p (s n)"),
+        in_=grouped[:].rearrange("p s n t -> p (s n t)"),
+    )
+
+
+def tile_multiheadselfattention_pa_kernel(tc, x, W, q_out, k_out, v_out):
+    nc = tc.nc
+    with ExitStack() as ctx:
+        pools = {
+            "fixed": ctx.enter_context(tc.tile_pool(name="fixed", bufs=1)),
+            "w_rows": ctx.enter_context(tc.tile_pool(name="w_rows", bufs=6)),
+            "grouped": ctx.enter_context(tc.tile_pool(name="grouped", bufs=3)),
+            "w_mx": ctx.enter_context(tc.tile_pool(name="w_mx", bufs=3)),
+            "terms": ctx.enter_context(tc.tile_pool(name="terms", bufs=4)),
+            "result": ctx.enter_context(tc.tile_pool(name="result", bufs=3)),
+            "flipped": ctx.enter_context(tc.psum_pool(name="flipped", bufs=3)),
+            "product": ctx.enter_context(tc.psum_pool(name="product", bufs=5)),
+        }
+        fixed = pools["fixed"]
+
+        column_tiles = []
+        for half in range(H // HEADS):
+            for part, dest in ((QUERY, q_out), (VALUE, v_out), (KEY, k_out)):
+                column_tiles.append((part, half, dest))
+
+        x_rows = fixed.tile([P, J, D], BF16)
+        x_view = x.rearrange("b (g j) c -> b g j c", j=J)
+
+        def load_x(tokens):
+            for b in range(B):
+                nc.sync.dma_start(out=x_rows[b:P:B, tokens, :], in_=x_view[b, :, tokens, :])
+
+        w_tiles = []
+
+        def load_w(part, half):
+            first_row = part * H * DH + half * N_TILE
+            w_rows = pools["w_rows"].tile([P, 2, 2, D], BF16)
+            nc.sync.dma_start(
+                out=w_rows[:].rearrange("p g e c -> p g (e c)"),
+                in_=W[first_row : first_row + N_TILE, :].rearrange("(g p e) c -> p g (e c)", g=2, e=2),
+            )
+            w_tiles.append(w_rows)
+
+        load_w(column_tiles[0][0], column_tiles[0][1])
+        load_x(slice(0, J // 2))
+        load_x(slice(J // 2, J))
+        for part, half, dest in column_tiles[1:]:
+            load_w(part, half)
+
+        identity = fixed.tile([P, P], F32)
+        make_identity(nc, identity[:])
+        table = build_rotation_table(nc, fixed)
+
+        x_codes = fixed.tile([P, J, PASSES, P], U32, align_bytes=64)
+        x_scales = fixed.tile([P, J, PASSES, P], U8, align_bytes=64)
+
+        def quantise_x(j):
+            quantise_rows(
+                nc, pools, identity, [x_rows[:, j, :].bitcast(F32)], x_codes[:, j], x_scales[:, j]
+            )
+
+        w_operands = []
+
+        def quantise_w(tile_index):
+            w_rows = w_tiles[tile_index]
+            w_codes = pools["w_mx"].tile([P, PASSES, N_TILE], U32, align_bytes=64)
+            w_scales = pools["w_mx"].tile([P, PASSES, N_TILE], U8, align_bytes=64)
+            blocks = []
+            for parity in range(2):
+                for group in range(2):
+                    blocks.append(w_rows[:, group, parity, :].bitcast(F32))
+            quantise_rows(nc, pools, identity, blocks, w_codes[:], w_scales[:])
+            w_operands.append((w_codes, w_scales))
+
+        def multiply(tile_index, result, j):
+            part, half, dest = column_tiles[tile_index]
+            w_codes, w_scales = w_operands[tile_index]
+            product = pools["product"].tile([P, 2, HEADS, PAIRS], F32)
+            for s in range(PASSES):
+                nc.tensor.matmul_mx(
+                    out=product[:].rearrange("p e h i -> p (e h i)"),
+                    lhsT=x_codes[:, j, s, :].bitcast(FP8X4),
+                    lhsT_scale=x_scales[:, j, s, :],
+                    rhs=w_codes[:, s, :].bitcast(FP8X4),
+                    rhs_scale=w_scales[:, s, :],
+                    start=(s == 0),
+                    stop=(s == PASSES - 1),
+                )
+            if part == VALUE:
+                nc.scalar.copy(
+                    out=result[:, :, j, :].rearrange("p h (i e) -> p h i e", e=2),
+                    in_=product[:].rearrange("p e h i -> p h i e"),
+                )
+            else:
+                shape = [P, 2, HEADS, PAIRS, 2]
+                terms = pools["terms"].tile(shape, F32)
+                nc.vector.tensor_tensor(
+                    out=terms[:],
+                    in0=product[:].unsqueeze(4).to_broadcast(shape),
+                    in1=table[:, j].unsqueeze(2).to_broadcast(shape),
+                    op=ALU.mult,
+                )
+                nc.gpsimd.tensor_tensor(
+                    out=result[:, :, j, :],
+                    in0=terms[:, 0].rearrange("p h i r -> p h (i r)"),
+                    in1=terms[:, 1].rearrange("p h i r -> p h (i r)"),
+                    op=ALU.add,
+                )
+
+        def store(tile_index, result, tokens):
+            part, half, dest = column_tiles[tile_index]
+            heads = slice(half * HEADS, (half + 1) * HEADS)
+            for b in range(B):
+                nc.sync.dma_start(
+                    out=dest[b, heads].rearrange("h (g j) d -> g h j d", j=J)[:, :, tokens, :],
+                    in_=result[b:P:B, :, tokens, :],
+                )
+
+        last = len(column_tiles) - 1
+        first_half, second_half = slice(0, J // 2), slice(J // 2, J)
+        quantise_w(0)
+        for j in range(J)[first_half]:
+            quantise_x(j)
+        for tile_index in range(len(column_tiles)):
+            result = pools["result"].tile([P, HEADS, J, DH], F32)
+            for j in range(J)[first_half]:
+                multiply(tile_index, result, j)
+            if tile_index == 0:
+                for j in range(J)[second_half]:
+                    quantise_x(j)
+            if tile_index < last:
+                quantise_w(tile_index + 1)
+            else:
+                store(tile_index, result, first_half)
+            for j in range(J)[second_half]:
+                multiply(tile_index, result, j)
+            store(tile_index, result, slice(0, J) if tile_index < last else second_half)

@@ -35,11 +35,17 @@ TURN_HI = 6.28125
 TURN_LO = 2.0 * math.pi - TURN_HI
 
 
-def build_rotation_table(nc, pool):
-    partition = pool.tile([P, 1], I32)
-    nc.gpsimd.iota(partition[:], pattern=[[0, 1]], base=0, channel_multiplier=1)
-    token = pool.tile([P, J], I32)
-    nc.gpsimd.iota(token[:], pattern=[[1, J]], base=0, channel_multiplier=0)
+def build_rotation_table(nc, pool, partition, token):
+    frequency = pool.tile([P, PAIRS], F32)
+    nc.vector.memset(frequency[:, 0:1], 1.0)
+    have = 1
+    while have < PAIRS:
+        nc.vector.tensor_scalar_mul(
+            out=frequency[:, have : 2 * have],
+            in0=frequency[:, 0:have],
+            scalar1=THETA ** (-2.0 * have / DH),
+        )
+        have *= 2
     first_int = pool.tile([P, 1], I32)
     nc.vector.tensor_scalar(
         out=first_int[:],
@@ -55,20 +61,9 @@ def build_rotation_table(nc, pool):
     nc.vector.tensor_copy(out=position[:], in_=token[:])
     nc.vector.tensor_scalar_add(out=position[:], in0=position[:], scalar1=first[:, 0:1])
 
-    frequency = pool.tile([P, PAIRS], F32)
-    nc.vector.memset(frequency[:, 0:1], 1.0)
-    have = 1
-    while have < PAIRS:
-        nc.vector.tensor_scalar_mul(
-            out=frequency[:, have : 2 * have],
-            in0=frequency[:, 0:have],
-            scalar1=THETA ** (-2.0 * have / DH),
-        )
-        have *= 2
-
-    angle = pool.tile([P, J, PAIRS], F32)
+    raw_angle = pool.tile([P, J, PAIRS], F32)
     nc.vector.tensor_tensor(
-        out=angle[:],
+        out=raw_angle[:],
         in0=position[:].unsqueeze(2).to_broadcast([P, J, PAIRS]),
         in1=frequency[:].unsqueeze(1).to_broadcast([P, J, PAIRS]),
         op=ALU.mult,
@@ -76,80 +71,56 @@ def build_rotation_table(nc, pool):
 
     turns = pool.tile([P, J, PAIRS], F32)
     nc.vector.tensor_scalar(
-        out=turns[:], in0=angle[:], scalar1=0.5 / math.pi, scalar2=ROUND, op0=ALU.mult, op1=ALU.add
+        out=turns[:], in0=raw_angle[:], scalar1=0.5 / math.pi, scalar2=ROUND, op0=ALU.mult, op1=ALU.add
     )
     nc.vector.tensor_scalar_add(out=turns[:], in0=turns[:], scalar1=-ROUND)
-    for part_of_turn in (TURN_HI, TURN_LO):
-        nc.vector.scalar_tensor_tensor(
-            out=angle[:], in0=turns[:], scalar=-part_of_turn, in1=angle[:], op0=ALU.mult, op1=ALU.add
-        )
-
-    phase_int = pool.tile([P, 2, 2], I32)
-    nc.gpsimd.iota(phase_int[:], pattern=[[1, 2], [-1, 2]], base=0, channel_multiplier=0)
-    phase = pool.tile([P, 2, 2], F32)
-    nc.vector.tensor_scalar_mul(out=phase[:], in0=phase_int[:], scalar1=0.5 * math.pi)
-
-    table = pool.tile([P, J, 2, PAIRS, 2], F32)
-    for source in range(2):
-        nc.vector.tensor_tensor(
-            out=table[:, :, source],
-            in0=angle[:].unsqueeze(3).to_broadcast([P, J, PAIRS, 2]),
-            in1=phase[:, source].unsqueeze(1).unsqueeze(1).to_broadcast([P, J, PAIRS, 2]),
-            op=ALU.add,
-        )
-    nc.scalar.activation(out=table[:], in_=table[:], func=ACT.Sin, scale=0.5)
-    nc.vector.tensor_tensor(out=table[:], in0=table[:], in1=table[:], op=ALU.mult)
+    nc.vector.scalar_tensor_tensor(
+        out=raw_angle[:], in0=turns[:], scalar=-TURN_HI, in1=raw_angle[:], op0=ALU.mult, op1=ALU.add
+    )
+    phased = pool.tile([P, J, 3, PAIRS], F32)
+    angle = phased[:, :, 1, :]
+    nc.vector.scalar_tensor_tensor(
+        out=angle, in0=turns[:], scalar=-TURN_LO, in1=raw_angle[:], op0=ALU.mult, op1=ALU.add
+    )
+    for m in (0, 2):
+        nc.vector.tensor_scalar_add(out=phased[:, :, m, :], in0=angle, scalar1=(1 - m) * 0.5 * math.pi)
+    table = pool.tile([P, J, 3, PAIRS], F32)
+    nc.scalar.activation(out=table[:], in_=phased[:], func=ACT.Sin, scale=0.5)
+    nc.scalar.activation(out=table[:], in_=table[:], func=ACT.Square)
     nc.vector.tensor_scalar(
         out=table[:], in0=table[:], scalar1=-2.0, scalar2=1.0, op0=ALU.mult, op1=ALU.add
     )
     return table
 
 
-def quantise_rows(nc, pools, identity, blocks, codes, scales):
-    columns = P * len(blocks)
-    grouped = pools["grouped"].tile(
-        [P, PASSES, columns, PACK], BF16, align_bytes=64, tag="grouped%d" % columns
-    )
-    grouped_words = grouped[:].bitcast(F32)
-    for block, words in enumerate(blocks):
-        flipped = pools["flipped"].tile([P, CHUNKS, P], F32)
-        for s in range(PASSES):
-            for u in range(2):
-                nc.tensor.transpose(
-                    flipped[:, 2 * s + u, :],
-                    words[:, 2 * P * s + u : 2 * P * (s + 1) : 2],
-                    identity[:],
-                )
-        nc.scalar.copy(
-            out=grouped_words[:, :, block * P : (block + 1) * P, :],
-            in_=flipped[:].rearrange("p (s u) r -> p s r u", u=2),
+STORE_TOKENS, LAST_STORE_TOKENS = 4, 2
+
+
+def transpose_words(nc, bank, words, identity, s):
+    for u in range(2):
+        nc.tensor.transpose(
+            bank[:, u, :], words[:, 2 * P * s + u : 2 * P * (s + 1) : 2], identity[:]
         )
-    nc.vector.quantize_mx(
-        out=codes.rearrange("p s n -> p (s n)").bitcast(FP8X4),
-        scales=scales.rearrange("p s n -> p (s n)"),
-        in_=grouped[:].rearrange("p s n t -> p (s n t)"),
-    )
 
 
 def tile_multiheadselfattention_pa_kernel(tc, x, W, q_out, k_out, v_out):
     nc = tc.nc
     with ExitStack() as ctx:
-        pools = {
-            "fixed": ctx.enter_context(tc.tile_pool(name="fixed", bufs=1)),
-            "w_rows": ctx.enter_context(tc.tile_pool(name="w_rows", bufs=6)),
-            "grouped": ctx.enter_context(tc.tile_pool(name="grouped", bufs=3)),
-            "w_mx": ctx.enter_context(tc.tile_pool(name="w_mx", bufs=3)),
-            "terms": ctx.enter_context(tc.tile_pool(name="terms", bufs=4)),
-            "result": ctx.enter_context(tc.tile_pool(name="result", bufs=3)),
-            "flipped": ctx.enter_context(tc.psum_pool(name="flipped", bufs=3)),
-            "product": ctx.enter_context(tc.psum_pool(name="product", bufs=5)),
-        }
-        fixed = pools["fixed"]
+        fixed = ctx.enter_context(tc.tile_pool(name="fixed", bufs=1))
+        w_row_pool = ctx.enter_context(tc.tile_pool(name="w_rows", bufs=6))
+        grouped_pool = ctx.enter_context(tc.tile_pool(name="grouped", bufs=3))
+        w_mx = ctx.enter_context(tc.tile_pool(name="w_mx", bufs=6))
+        terms_pool = ctx.enter_context(tc.tile_pool(name="terms", bufs=4))
+        result_pool = ctx.enter_context(tc.tile_pool(name="result", bufs=4))
+        bank_pool = ctx.enter_context(tc.psum_pool(name="bank", bufs=8))
+        ctx.enter_context(tc.manual_schedule())
 
-        column_tiles = []
-        for half in range(H // HEADS):
-            for part, dest in ((QUERY, q_out), (VALUE, v_out), (KEY, k_out)):
-                column_tiles.append((part, half, dest))
+        tiles = [
+            (QUERY, 0, q_out), (KEY, 0, k_out), (VALUE, 0, v_out),
+            (QUERY, 1, q_out), (KEY, 1, k_out), (VALUE, 1, v_out),
+        ]
+        rotated = [t for t in range(len(tiles)) if tiles[t][0] != VALUE]
+        copied = [t for t in range(len(tiles)) if tiles[t][0] == VALUE]
 
         x_rows = fixed.tile([P, J, D], BF16)
         x_view = x.rearrange("b (g j) c -> b g j c", j=J)
@@ -162,104 +133,200 @@ def tile_multiheadselfattention_pa_kernel(tc, x, W, q_out, k_out, v_out):
 
         def load_w(part, half):
             first_row = part * H * DH + half * N_TILE
-            w_rows = pools["w_rows"].tile([P, 2, 2, D], BF16)
-            nc.sync.dma_start(
-                out=w_rows[:].rearrange("p g e c -> p g (e c)"),
-                in_=W[first_row : first_row + N_TILE, :].rearrange("(g p e) c -> p g (e c)", g=2, e=2),
-            )
+            w_rows = w_row_pool.tile([P, 2, 2, D], BF16)
+            for g in range(2):
+                row = first_row + g * 2 * P
+                nc.sync.dma_start(
+                    out=w_rows[:, g].rearrange("p e c -> p (e c)"),
+                    in_=W[row : row + 2 * P, :].rearrange("(p e) c -> p (e c)", e=2),
+                )
             w_tiles.append(w_rows)
 
-        load_w(column_tiles[0][0], column_tiles[0][1])
-        load_x(slice(0, J // 2))
-        load_x(slice(J // 2, J))
-        for part, half, dest in column_tiles[1:]:
+        load_x(slice(0, 2))
+        load_w(tiles[0][0], tiles[0][1])
+        load_x(slice(2, 4))
+        load_x(slice(4, J))
+        for part, half, dest in tiles[1:]:
             load_w(part, half)
 
+        partition = fixed.tile([P, 1], I32)
+        nc.gpsimd.iota(partition[:], pattern=[[0, 1]], base=0, channel_multiplier=1)
+        token = fixed.tile([P, J], I32)
+        nc.gpsimd.iota(token[:], pattern=[[1, J]], base=0, channel_multiplier=0)
         identity = fixed.tile([P, P], F32)
         make_identity(nc, identity[:])
-        table = build_rotation_table(nc, fixed)
+        table = build_rotation_table(nc, fixed, partition, token)
 
         x_codes = fixed.tile([P, J, PASSES, P], U32, align_bytes=64)
         x_scales = fixed.tile([P, J, PASSES, P], U8, align_bytes=64)
+        w_codes = {}
+        w_scales = {}
+        grouped_x = {}
+        grouped_w = {}
 
-        def quantise_x(j):
-            quantise_rows(
-                nc, pools, identity, [x_rows[:, j, :].bitcast(F32)], x_codes[:, j], x_scales[:, j]
+        def copy_out(on_vector, out, in_):
+            if on_vector:
+                nc.vector.tensor_copy(out=out, in_=in_)
+            else:
+                nc.scalar.copy(out=out, in_=in_)
+
+        def flip_x(pair, on_vector=(False, False)):
+            grouped = grouped_pool.tile([P, 2, PASSES, P, PACK], BF16, align_bytes=64, name="grouped_x")
+            for k in range(2):
+                bank = bank_pool.tile([P, PASSES, 2, P], F32, name="bank")
+                for s in range(PASSES):
+                    transpose_words(nc, bank[:, s], x_rows[:, 2 * pair + k, :].bitcast(F32), identity, s)
+                copy_out(
+                    on_vector[k], grouped[:, k].bitcast(F32), bank[:].rearrange("p s u r -> p s r u")
+                )
+            grouped_x[pair] = grouped
+
+        def quantise_x(pair):
+            pair_tokens = slice(2 * pair, 2 * pair + 2)
+            nc.vector.quantize_mx(
+                out=x_codes[:, pair_tokens].rearrange("p j s n -> p (j s n)").bitcast(FP8X4),
+                scales=x_scales[:, pair_tokens].rearrange("p j s n -> p (j s n)"),
+                in_=grouped_x[pair][:].rearrange("p j s n t -> p (j s n t)"),
             )
 
-        w_operands = []
+        def flip_w(t, on_vector=(False, False, False, False)):
+            grouped = grouped_pool.tile([P, PASSES, N_TILE, PACK], BF16, align_bytes=64, name="grouped_w")
+            words = grouped[:].bitcast(F32)
+            for group in range(2):
+                for parity in range(2):
+                    bank = bank_pool.tile([P, PASSES, 2, P], F32, name="bank")
+                    for s in range(PASSES):
+                        transpose_words(
+                            nc, bank[:, s], w_tiles[t][:, group, parity, :].bitcast(F32), identity, s
+                        )
+                    first = P * (2 * parity + group)
+                    copy_out(
+                        on_vector[2 * group + parity],
+                        words[:, :, first : first + P, :],
+                        bank[:].rearrange("p s u r -> p s r u"),
+                    )
+            grouped_w[t] = grouped
 
-        def quantise_w(tile_index):
-            w_rows = w_tiles[tile_index]
-            w_codes = pools["w_mx"].tile([P, PASSES, N_TILE], U32, align_bytes=64)
-            w_scales = pools["w_mx"].tile([P, PASSES, N_TILE], U8, align_bytes=64)
-            blocks = []
-            for parity in range(2):
-                for group in range(2):
-                    blocks.append(w_rows[:, group, parity, :].bitcast(F32))
-            quantise_rows(nc, pools, identity, blocks, w_codes[:], w_scales[:])
-            w_operands.append((w_codes, w_scales))
+        def quantise_w(t):
+            codes = w_mx.tile([P, PASSES, N_TILE], U32, align_bytes=64, name="codes")
+            scales = w_mx.tile([P, PASSES, N_TILE], U8, align_bytes=64, name="scales")
+            nc.vector.quantize_mx(
+                out=codes[:].rearrange("p s n -> p (s n)").bitcast(FP8X4),
+                scales=scales[:].rearrange("p s n -> p (s n)"),
+                in_=grouped_w[t][:].rearrange("p s n t -> p (s n t)"),
+            )
+            w_codes[t] = codes
+            w_scales[t] = scales
 
-        def multiply(tile_index, result, j):
-            part, half, dest = column_tiles[tile_index]
-            w_codes, w_scales = w_operands[tile_index]
-            product = pools["product"].tile([P, 2, HEADS, PAIRS], F32)
+        products = {}
+
+        def multiply(t, j):
+            product = bank_pool.tile([P, 2, HEADS, PAIRS], F32, name="bank")
             for s in range(PASSES):
                 nc.tensor.matmul_mx(
                     out=product[:].rearrange("p e h i -> p (e h i)"),
                     lhsT=x_codes[:, j, s, :].bitcast(FP8X4),
                     lhsT_scale=x_scales[:, j, s, :],
-                    rhs=w_codes[:, s, :].bitcast(FP8X4),
-                    rhs_scale=w_scales[:, s, :],
+                    rhs=w_codes[t][:, s, :].bitcast(FP8X4),
+                    rhs_scale=w_scales[t][:, s, :],
                     start=(s == 0),
                     stop=(s == PASSES - 1),
                 )
-            if part == VALUE:
-                nc.scalar.copy(
-                    out=result[:, :, j, :].rearrange("p h (i e) -> p h i e", e=2),
-                    in_=product[:].rearrange("p e h i -> p h i e"),
-                )
-            else:
-                shape = [P, 2, HEADS, PAIRS, 2]
-                terms = pools["terms"].tile(shape, F32)
-                nc.vector.tensor_tensor(
-                    out=terms[:],
-                    in0=product[:].unsqueeze(4).to_broadcast(shape),
-                    in1=table[:, j].unsqueeze(2).to_broadcast(shape),
-                    op=ALU.mult,
-                )
-                nc.gpsimd.tensor_tensor(
-                    out=result[:, :, j, :],
-                    in0=terms[:, 0].rearrange("p h i r -> p h (i r)"),
-                    in1=terms[:, 1].rearrange("p h i r -> p h (i r)"),
-                    op=ALU.add,
-                )
+            products[t, j] = product
 
-        def store(tile_index, result, tokens):
-            part, half, dest = column_tiles[tile_index]
+        results = {}
+
+        def result_of(t, j):
+            if j == 0:
+                results[t] = result_pool.tile([P, HEADS, J, DH], F32, name="result")
+            return results[t]
+
+        def store(t, tokens):
+            part, half, dest = tiles[t]
             heads = slice(half * HEADS, (half + 1) * HEADS)
             for b in range(B):
                 nc.sync.dma_start(
                     out=dest[b, heads].rearrange("h (g j) d -> g h j d", j=J)[:, :, tokens, :],
-                    in_=result[b:P:B, :, tokens, :],
+                    in_=results[t][b:P:B, :, tokens, :],
                 )
 
-        last = len(column_tiles) - 1
-        first_half, second_half = slice(0, J // 2), slice(J // 2, J)
+        def finish(t, j):
+            tokens = LAST_STORE_TOKENS if t == rotated[-1] else STORE_TOKENS
+            if j % tokens == tokens - 1:
+                store(t, slice(j + 1 - tokens, j + 1))
+
+        def rotate(t, j):
+            product = products[t, j]
+            result = result_of(t, j)
+            shape = [P, 2, HEADS, PAIRS, 2]
+            terms = terms_pool.tile(shape, F32, name="terms")
+            for source in range(2):
+                factors = table[:, j, 1 - source : 3 - source, :].rearrange("p r i -> p i r")
+                nc.vector.tensor_tensor(
+                    out=terms[:, source],
+                    in0=product[:, source].unsqueeze(3).to_broadcast(shape[:1] + shape[2:]),
+                    in1=factors.unsqueeze(1).to_broadcast(shape[:1] + shape[2:]),
+                    op=ALU.mult,
+                )
+            adder = nc.vector if (t, j) == (rotated[-1], J - 1) else nc.gpsimd
+            adder.tensor_tensor(
+                out=result[:, :, j, :],
+                in0=terms[:, 0].rearrange("p h i r -> p h (i r)"),
+                in1=terms[:, 1].rearrange("p h i r -> p h (i r)"),
+                op=ALU.add,
+            )
+            finish(t, j)
+
+        def copy_value(t, j):
+            product = products[t, j]
+            result = result_of(t, j)
+            nc.scalar.copy(
+                out=result[:, :, j, :].rearrange("p h (i e) -> p h i e", e=2),
+                in_=product[:].rearrange("p e h i -> p h i e"),
+            )
+            finish(t, j)
+
+        steps = [(t, j) for t in rotated for j in range(J)]
+        copies = [(t, j) for t in copied for j in range(J)]
+        flip_x(0, (True, False))
+        flip_w(0, (True, False, True, False))
+        quantise_x(0)
         quantise_w(0)
-        for j in range(J)[first_half]:
-            quantise_x(j)
-        for tile_index in range(len(column_tiles)):
-            result = pools["result"].tile([P, HEADS, J, DH], F32)
-            for j in range(J)[first_half]:
-                multiply(tile_index, result, j)
-            if tile_index == 0:
-                for j in range(J)[second_half]:
-                    quantise_x(j)
-            if tile_index < last:
-                quantise_w(tile_index + 1)
+        flip_x(1)
+        multiply(0, 0)
+        multiply(0, 1)
+        flip_x(2)
+        rotate(0, 0)
+        quantise_x(1)
+        multiply(0, 2)
+        flip_x(3)
+        rotate(0, 1)
+        quantise_x(2)
+        multiply(0, 3)
+        done = 2
+        made = 4
+        for n in range(1, len(tiles)):
+            flip_w(n, (False, False, False, False))
+            rotate(*steps[done])
+            done += 1
+            if n == 1:
+                quantise_x(3)
             else:
-                store(tile_index, result, first_half)
-            for j in range(J)[second_half]:
-                multiply(tile_index, result, j)
-            store(tile_index, result, slice(0, J) if tile_index < last else second_half)
+                quantise_w(n - 1)
+            multiply(*steps[made])
+            made += 1
+        rotate(*steps[done])
+        done += 1
+        quantise_w(len(tiles) - 1)
+        copied_count = 0
+        left = len(steps) - done
+        for r in range(done, len(steps)):
+            while made < min(r + 3, len(steps)):
+                multiply(*steps[made])
+                made += 1
+            want = (r + 1 - done) * len(copies) // left
+            while copied_count < want:
+                multiply(*copies[copied_count])
+                copy_value(*copies[copied_count])
+                copied_count += 1
+            rotate(*steps[r])

@@ -35,12 +35,12 @@ TURN_HI = 6.28125
 TURN_LO = 2.0 * math.pi - TURN_HI
 
 
-def build_rotation_table(nc, pool, partition, token):
+def build_angles(nc, pool, partition, token):
     frequency = pool.tile([P, PAIRS], F32)
-    nc.vector.memset(frequency[:, 0:1], 1.0)
+    nc.gpsimd.memset(frequency[:, 0:1], 1.0)
     have = 1
     while have < PAIRS:
-        nc.vector.tensor_scalar_mul(
+        nc.gpsimd.tensor_scalar_mul(
             out=frequency[:, have : 2 * have],
             in0=frequency[:, 0:have],
             scalar1=THETA ** (-2.0 * have / DH),
@@ -84,6 +84,10 @@ def build_rotation_table(nc, pool, partition, token):
     )
     for m in (0, 2):
         nc.vector.tensor_scalar_add(out=phased[:, :, m, :], in0=angle, scalar1=(1 - m) * 0.5 * math.pi)
+    return phased
+
+
+def finish_table(nc, pool, phased):
     table = pool.tile([P, J, 3, PAIRS], F32)
     nc.scalar.activation(out=table[:], in_=phased[:], func=ACT.Sin, scale=0.5)
     nc.scalar.activation(out=table[:], in_=table[:], func=ACT.Square)
@@ -93,7 +97,7 @@ def build_rotation_table(nc, pool, partition, token):
     return table
 
 
-STORE_TOKENS, LAST_STORE_TOKENS = 4, 2
+STORE_TOKENS = 4
 
 
 def transpose_words(nc, bank, words, identity, s):
@@ -111,7 +115,7 @@ def tile_multiheadselfattention_pa_kernel(tc, x, W, q_out, k_out, v_out):
         grouped_pool = ctx.enter_context(tc.tile_pool(name="grouped", bufs=3))
         w_mx = ctx.enter_context(tc.tile_pool(name="w_mx", bufs=6))
         terms_pool = ctx.enter_context(tc.tile_pool(name="terms", bufs=4))
-        result_pool = ctx.enter_context(tc.tile_pool(name="result", bufs=4))
+        result_pool = ctx.enter_context(tc.tile_pool(name="result", bufs=6))
         bank_pool = ctx.enter_context(tc.psum_pool(name="bank", bufs=8))
         ctx.enter_context(tc.manual_schedule())
 
@@ -122,12 +126,16 @@ def tile_multiheadselfattention_pa_kernel(tc, x, W, q_out, k_out, v_out):
         rotated = [t for t in range(len(tiles)) if tiles[t][0] != VALUE]
         copied = [t for t in range(len(tiles)) if tiles[t][0] == VALUE]
 
-        x_rows = fixed.tile([P, J, D], BF16)
+        x_pairs = [
+            fixed.tile([P, 2, D], BF16, name="x_pair%d" % pair) for pair in range(J // 2)
+        ]
         x_view = x.rearrange("b (g j) c -> b g j c", j=J)
 
-        def load_x(tokens):
+        def load_x(pair):
             for b in range(B):
-                nc.sync.dma_start(out=x_rows[b:P:B, tokens, :], in_=x_view[b, :, tokens, :])
+                nc.sync.dma_start(
+                    out=x_pairs[pair][b:P:B], in_=x_view[b, :, 2 * pair : 2 * pair + 2, :]
+                )
 
         w_tiles = []
 
@@ -142,10 +150,10 @@ def tile_multiheadselfattention_pa_kernel(tc, x, W, q_out, k_out, v_out):
                 )
             w_tiles.append(w_rows)
 
-        load_x(slice(0, 2))
+        load_x(0)
         load_w(tiles[0][0], tiles[0][1])
-        load_x(slice(2, 4))
-        load_x(slice(4, J))
+        for pair in range(1, J // 2):
+            load_x(pair)
         for part, half, dest in tiles[1:]:
             load_w(part, half)
 
@@ -155,7 +163,7 @@ def tile_multiheadselfattention_pa_kernel(tc, x, W, q_out, k_out, v_out):
         nc.gpsimd.iota(token[:], pattern=[[1, J]], base=0, channel_multiplier=0)
         identity = fixed.tile([P, P], F32)
         make_identity(nc, identity[:])
-        table = build_rotation_table(nc, fixed, partition, token)
+        phased = build_angles(nc, fixed, partition, token)
 
         x_codes = fixed.tile([P, J, PASSES, P], U32, align_bytes=64)
         x_scales = fixed.tile([P, J, PASSES, P], U8, align_bytes=64)
@@ -175,7 +183,7 @@ def tile_multiheadselfattention_pa_kernel(tc, x, W, q_out, k_out, v_out):
             for k in range(2):
                 bank = bank_pool.tile([P, PASSES, 2, P], F32, name="bank")
                 for s in range(PASSES):
-                    transpose_words(nc, bank[:, s], x_rows[:, 2 * pair + k, :].bitcast(F32), identity, s)
+                    transpose_words(nc, bank[:, s], x_pairs[pair][:, k, :].bitcast(F32), identity, s)
                 copy_out(
                     on_vector[k], grouped[:, k].bitcast(F32), bank[:].rearrange("p s u r -> p s r u")
                 )
@@ -237,9 +245,9 @@ def tile_multiheadselfattention_pa_kernel(tc, x, W, q_out, k_out, v_out):
         results = {}
 
         def result_of(t, j):
-            if j == 0:
-                results[t] = result_pool.tile([P, HEADS, J, DH], F32, name="result")
-            return results[t]
+            if j % STORE_TOKENS == 0:
+                results[t] = result_pool.tile([P, HEADS, STORE_TOKENS, DH], F32, name="result")
+            return results[t][:, :, j % STORE_TOKENS, :]
 
         def store(t, tokens):
             part, half, dest = tiles[t]
@@ -247,13 +255,12 @@ def tile_multiheadselfattention_pa_kernel(tc, x, W, q_out, k_out, v_out):
             for b in range(B):
                 nc.sync.dma_start(
                     out=dest[b, heads].rearrange("h (g j) d -> g h j d", j=J)[:, :, tokens, :],
-                    in_=results[t][b:P:B, :, tokens, :],
+                    in_=results[t][b:P:B],
                 )
 
         def finish(t, j):
-            tokens = LAST_STORE_TOKENS if t == rotated[-1] else STORE_TOKENS
-            if j % tokens == tokens - 1:
-                store(t, slice(j + 1 - tokens, j + 1))
+            if j % STORE_TOKENS == STORE_TOKENS - 1:
+                store(t, slice(j + 1 - STORE_TOKENS, j + 1))
 
         def rotate(t, j):
             product = products[t, j]
@@ -270,7 +277,7 @@ def tile_multiheadselfattention_pa_kernel(tc, x, W, q_out, k_out, v_out):
                 )
             adder = nc.vector if (t, j) == (rotated[-1], J - 1) else nc.gpsimd
             adder.tensor_tensor(
-                out=result[:, :, j, :],
+                out=result,
                 in0=terms[:, 0].rearrange("p h i r -> p h (i r)"),
                 in1=terms[:, 1].rearrange("p h i r -> p h (i r)"),
                 op=ALU.add,
@@ -281,17 +288,18 @@ def tile_multiheadselfattention_pa_kernel(tc, x, W, q_out, k_out, v_out):
             product = products[t, j]
             result = result_of(t, j)
             nc.scalar.copy(
-                out=result[:, :, j, :].rearrange("p h (i e) -> p h i e", e=2),
+                out=result.rearrange("p h (i e) -> p h i e", e=2),
                 in_=product[:].rearrange("p e h i -> p h i e"),
             )
             finish(t, j)
 
         steps = [(t, j) for t in rotated for j in range(J)]
         copies = [(t, j) for t in copied for j in range(J)]
-        flip_x(0, (True, False))
-        flip_w(0, (True, False, True, False))
+        flip_x(0)
+        flip_w(0, (False, True, False, True))
         quantise_x(0)
         quantise_w(0)
+        table = finish_table(nc, fixed, phased)
         flip_x(1)
         multiply(0, 0)
         multiply(0, 1)
@@ -306,7 +314,7 @@ def tile_multiheadselfattention_pa_kernel(tc, x, W, q_out, k_out, v_out):
         done = 2
         made = 4
         for n in range(1, len(tiles)):
-            flip_w(n, (False, False, False, False))
+            flip_w(n)
             rotate(*steps[done])
             done += 1
             if n == 1:

@@ -36,68 +36,62 @@ TURN_LO = 2.0 * math.pi - TURN_HI
 
 
 def build_angles(nc, pool, partition, token):
-    frequency = pool.tile([P, PAIRS], F32)
-    nc.gpsimd.memset(frequency[:, 0:1], 1.0)
-    have = 1
-    while have < PAIRS:
-        nc.gpsimd.tensor_scalar_mul(
-            out=frequency[:, have : 2 * have],
-            in0=frequency[:, 0:have],
-            scalar1=THETA ** (-2.0 * have / DH),
-        )
-        have *= 2
-    first_int = pool.tile([P, 1], I32)
+    first = pool.tile([P, 1], I32)
     nc.vector.tensor_scalar(
-        out=first_int[:],
+        out=first[:],
         in0=partition[:],
         scalar1=B_BITS,
         scalar2=J_BITS,
         op0=ALU.logical_shift_right,
         op1=ALU.logical_shift_left,
     )
-    first = pool.tile([P, 1], F32)
-    nc.vector.tensor_copy(out=first[:], in_=first_int[:])
-    position = pool.tile([P, J], F32)
-    nc.vector.tensor_copy(out=position[:], in_=token[:])
-    nc.vector.tensor_scalar_add(out=position[:], in0=position[:], scalar1=first[:, 0:1])
-
-    raw_angle = pool.tile([P, J, PAIRS], F32)
-    nc.vector.tensor_tensor(
-        out=raw_angle[:],
-        in0=position[:].unsqueeze(2).to_broadcast([P, J, PAIRS]),
-        in1=frequency[:].unsqueeze(1).to_broadcast([P, J, PAIRS]),
-        op=ALU.mult,
-    )
+    angle = pool.tile([P, J, PAIRS], F32)
+    nc.vector.tensor_scalar_add(out=angle[:, :, 0], in0=token[:], scalar1=first[:, 0:1])
+    have = 1
+    while have < PAIRS:
+        nc.vector.tensor_scalar_mul(
+            out=angle[:, :, have : 2 * have],
+            in0=angle[:, :, 0:have],
+            scalar1=THETA ** (-2.0 * have / DH),
+        )
+        have *= 2
 
     turns = pool.tile([P, J, PAIRS], F32)
     nc.vector.tensor_scalar(
-        out=turns[:], in0=raw_angle[:], scalar1=0.5 / math.pi, scalar2=ROUND, op0=ALU.mult, op1=ALU.add
+        out=turns[:], in0=angle[:], scalar1=0.5 / math.pi, scalar2=ROUND, op0=ALU.mult, op1=ALU.add
     )
     nc.vector.tensor_scalar_add(out=turns[:], in0=turns[:], scalar1=-ROUND)
     nc.vector.scalar_tensor_tensor(
-        out=raw_angle[:], in0=turns[:], scalar=-TURN_HI, in1=raw_angle[:], op0=ALU.mult, op1=ALU.add
+        out=angle[:], in0=turns[:], scalar=-TURN_HI, in1=angle[:], op0=ALU.mult, op1=ALU.add
     )
     phased = pool.tile([P, J, 3, PAIRS], F32)
-    angle = phased[:, :, 1, :]
     nc.vector.scalar_tensor_tensor(
-        out=angle, in0=turns[:], scalar=-TURN_LO, in1=raw_angle[:], op0=ALU.mult, op1=ALU.add
+        out=phased[:, :, 1, :], in0=turns[:], scalar=-TURN_LO, in1=angle[:], op0=ALU.mult, op1=ALU.add
     )
     for m in (0, 2):
-        nc.vector.tensor_scalar_add(out=phased[:, :, m, :], in0=angle, scalar1=(1 - m) * 0.5 * math.pi)
+        nc.vector.tensor_scalar_add(
+            out=phased[:, :, m, :], in0=phased[:, :, 1, :], scalar1=(1 - m) * 0.5 * math.pi
+        )
     return phased
 
 
-def finish_table(nc, pool, phased):
-    table = pool.tile([P, J, 3, PAIRS], F32)
-    nc.scalar.activation(out=table[:], in_=phased[:], func=ACT.Sin, scale=0.5)
-    nc.scalar.activation(out=table[:], in_=table[:], func=ACT.Square)
-    nc.vector.tensor_scalar(
-        out=table[:], in0=table[:], scalar1=-2.0, scalar2=1.0, op0=ALU.mult, op1=ALU.add
-    )
+def square_sines(nc, pool, phased):
+    sines = pool.tile([P, J, 3, PAIRS], F32)
+    nc.scalar.activation(out=sines[:], in_=phased[:], func=ACT.Sin, scale=0.5)
+    table = pool.tile([P, J, 2, PAIRS, 2], F32)
+    for source in range(2):
+        nc.scalar.activation(
+            out=table[:, :, source],
+            in_=sines[:, :, 1 - source : 3 - source, :].rearrange("p j r i -> p j i r"),
+            func=ACT.Square,
+        )
     return table
 
 
-STORE_TOKENS = 4
+def finish_table(nc, table):
+    nc.vector.tensor_scalar(
+        out=table[:], in0=table[:], scalar1=-2.0, scalar2=1.0, op0=ALU.mult, op1=ALU.add
+    )
 
 
 def transpose_words(nc, bank, words, identity, s):
@@ -157,6 +151,8 @@ def tile_multiheadselfattention_pa_kernel(tc, x, W, q_out, k_out, v_out):
         for part, half, dest in tiles[1:]:
             load_w(part, half)
 
+        zeros = fixed.tile([P, N_TILE], BF16)
+        nc.vector.memset(zeros[:].bitcast(F32), 0.0)
         partition = fixed.tile([P, 1], I32)
         nc.gpsimd.iota(partition[:], pattern=[[0, 1]], base=0, channel_multiplier=1)
         token = fixed.tile([P, J], I32)
@@ -171,6 +167,11 @@ def tile_multiheadselfattention_pa_kernel(tc, x, W, q_out, k_out, v_out):
         w_scales = {}
         grouped_x = {}
         grouped_w = {}
+
+        def warm_up(count):
+            bank = bank_pool.tile([P, N_TILE], F32, name="bank")
+            for _ in range(count):
+                nc.tensor.matmul(bank[:], lhsT=zeros[:, 0:P], rhs=zeros[:], start=True, stop=True)
 
         def copy_out(on_vector, out, in_):
             if on_vector:
@@ -197,23 +198,24 @@ def tile_multiheadselfattention_pa_kernel(tc, x, W, q_out, k_out, v_out):
                 in_=grouped_x[pair][:].rearrange("p j s n t -> p (j s n t)"),
             )
 
-        def flip_w(t, on_vector=(False, False, False, False)):
-            grouped = grouped_pool.tile([P, PASSES, N_TILE, PACK], BF16, align_bytes=64, name="grouped_w")
-            words = grouped[:].bitcast(F32)
-            for group in range(2):
-                for parity in range(2):
-                    bank = bank_pool.tile([P, PASSES, 2, P], F32, name="bank")
-                    for s in range(PASSES):
-                        transpose_words(
-                            nc, bank[:, s], w_tiles[t][:, group, parity, :].bitcast(F32), identity, s
-                        )
-                    first = P * (2 * parity + group)
-                    copy_out(
-                        on_vector[2 * group + parity],
-                        words[:, :, first : first + P, :],
-                        bank[:].rearrange("p s u r -> p s r u"),
+        def flip_w(t, group, on_vector=(False, False)):
+            if group == 0:
+                grouped_w[t] = grouped_pool.tile(
+                    [P, PASSES, N_TILE, PACK], BF16, align_bytes=64, name="grouped_w"
+                )
+            words = grouped_w[t][:].bitcast(F32)
+            for parity in range(2):
+                bank = bank_pool.tile([P, PASSES, 2, P], F32, name="bank")
+                for s in range(PASSES):
+                    transpose_words(
+                        nc, bank[:, s], w_tiles[t][:, group, parity, :].bitcast(F32), identity, s
                     )
-            grouped_w[t] = grouped
+                first = P * (2 * parity + group)
+                copy_out(
+                    on_vector[parity],
+                    words[:, :, first : first + P, :],
+                    bank[:].rearrange("p s u r -> p s r u"),
+                )
 
         def quantise_w(t):
             codes = w_mx.tile([P, PASSES, N_TILE], U32, align_bytes=64, name="codes")
@@ -244,10 +246,17 @@ def tile_multiheadselfattention_pa_kernel(tc, x, W, q_out, k_out, v_out):
 
         results = {}
 
+        def store_tokens(t, j):
+            size = J // 4 if t == rotated[-1] and j >= J // 2 else J // 2
+            return slice(j - j % size, j - j % size + size)
+
         def result_of(t, j):
-            if j % STORE_TOKENS == 0:
-                results[t] = result_pool.tile([P, HEADS, STORE_TOKENS, DH], F32, name="result")
-            return results[t][:, :, j % STORE_TOKENS, :]
+            tokens = store_tokens(t, j)
+            if j == tokens.start:
+                results[t] = result_pool.tile(
+                    [P, HEADS, tokens.stop - tokens.start, DH], F32, name="result"
+                )
+            return results[t][:, :, j - tokens.start, :]
 
         def store(t, tokens):
             part, half, dest = tiles[t]
@@ -259,22 +268,20 @@ def tile_multiheadselfattention_pa_kernel(tc, x, W, q_out, k_out, v_out):
                 )
 
         def finish(t, j):
-            if j % STORE_TOKENS == STORE_TOKENS - 1:
-                store(t, slice(j + 1 - STORE_TOKENS, j + 1))
+            if j == store_tokens(t, j).stop - 1:
+                store(t, store_tokens(t, j))
 
         def rotate(t, j):
             product = products[t, j]
             result = result_of(t, j)
             shape = [P, 2, HEADS, PAIRS, 2]
             terms = terms_pool.tile(shape, F32, name="terms")
-            for source in range(2):
-                factors = table[:, j, 1 - source : 3 - source, :].rearrange("p r i -> p i r")
-                nc.vector.tensor_tensor(
-                    out=terms[:, source],
-                    in0=product[:, source].unsqueeze(3).to_broadcast(shape[:1] + shape[2:]),
-                    in1=factors.unsqueeze(1).to_broadcast(shape[:1] + shape[2:]),
-                    op=ALU.mult,
-                )
+            nc.vector.tensor_tensor(
+                out=terms[:],
+                in0=product[:].unsqueeze(4).to_broadcast(shape),
+                in1=table[:, j].unsqueeze(2).to_broadcast(shape),
+                op=ALU.mult,
+            )
             adder = nc.vector if (t, j) == (rotated[-1], J - 1) else nc.gpsimd
             adder.tensor_tensor(
                 out=result,
@@ -295,11 +302,14 @@ def tile_multiheadselfattention_pa_kernel(tc, x, W, q_out, k_out, v_out):
 
         steps = [(t, j) for t in rotated for j in range(J)]
         copies = [(t, j) for t in copied for j in range(J)]
+        warm_up(7)
         flip_x(0)
-        flip_w(0, (False, True, False, True))
+        flip_w(0, 0, (True, True))
+        table = square_sines(nc, fixed, phased)
+        flip_w(0, 1, (True, False))
         quantise_x(0)
         quantise_w(0)
-        table = finish_table(nc, fixed, phased)
+        finish_table(nc, table)
         flip_x(1)
         multiply(0, 0)
         multiply(0, 1)
@@ -314,15 +324,16 @@ def tile_multiheadselfattention_pa_kernel(tc, x, W, q_out, k_out, v_out):
         done = 2
         made = 4
         for n in range(1, len(tiles)):
-            flip_w(n)
-            rotate(*steps[done])
-            done += 1
-            if n == 1:
-                quantise_x(3)
-            else:
-                quantise_w(n - 1)
-            multiply(*steps[made])
-            made += 1
+            for group in range(2):
+                flip_w(n, group)
+                rotate(*steps[done])
+                done += 1
+                if n == 1 and group == 0:
+                    quantise_x(3)
+                if n > 1 and group == 0:
+                    quantise_w(n - 1)
+                multiply(*steps[made])
+                made += 1
         rotate(*steps[done])
         done += 1
         quantise_w(len(tiles) - 1)

@@ -75,22 +75,19 @@ def build_angles(nc, pool, partition, token):
     return phased
 
 
-def square_sines(nc, pool, phased):
-    sines = pool.tile([P, J, 3, PAIRS], F32)
-    nc.scalar.activation(out=sines[:], in_=phased[:], func=ACT.Sin, scale=0.5)
-    table = pool.tile([P, J, 2, PAIRS, 2], F32)
+def square_sines(nc, sines, table, phased, tokens):
+    nc.scalar.activation(out=sines[:, tokens], in_=phased[:, tokens], func=ACT.Sin, scale=0.5)
     for source in range(2):
         nc.scalar.activation(
-            out=table[:, :, source],
-            in_=sines[:, :, 1 - source : 3 - source, :].rearrange("p j r i -> p j i r"),
+            out=table[:, tokens, source],
+            in_=sines[:, tokens, 1 - source : 3 - source, :].rearrange("p j r i -> p j i r"),
             func=ACT.Square,
         )
-    return table
 
 
-def finish_table(nc, table):
+def finish_table(nc, table, tokens):
     nc.vector.tensor_scalar(
-        out=table[:], in0=table[:], scalar1=-2.0, scalar2=1.0, op0=ALU.mult, op1=ALU.add
+        out=table[:, tokens], in0=table[:, tokens], scalar1=-2.0, scalar2=1.0, op0=ALU.mult, op1=ALU.add
     )
 
 
@@ -151,8 +148,6 @@ def tile_multiheadselfattention_pa_kernel(tc, x, W, q_out, k_out, v_out):
         for part, half, dest in tiles[1:]:
             load_w(part, half)
 
-        zeros = fixed.tile([P, N_TILE], BF16)
-        nc.vector.memset(zeros[:].bitcast(F32), 0.0)
         partition = fixed.tile([P, 1], I32)
         nc.gpsimd.iota(partition[:], pattern=[[0, 1]], base=0, channel_multiplier=1)
         token = fixed.tile([P, J], I32)
@@ -160,6 +155,8 @@ def tile_multiheadselfattention_pa_kernel(tc, x, W, q_out, k_out, v_out):
         identity = fixed.tile([P, P], F32)
         make_identity(nc, identity[:])
         phased = build_angles(nc, fixed, partition, token)
+        sines = fixed.tile([P, J, 3, PAIRS], F32)
+        table = fixed.tile([P, J, 2, PAIRS, 2], F32)
 
         x_codes = fixed.tile([P, J, PASSES, P], U32, align_bytes=64)
         x_scales = fixed.tile([P, J, PASSES, P], U8, align_bytes=64)
@@ -167,11 +164,6 @@ def tile_multiheadselfattention_pa_kernel(tc, x, W, q_out, k_out, v_out):
         w_scales = {}
         grouped_x = {}
         grouped_w = {}
-
-        def warm_up(count):
-            bank = bank_pool.tile([P, N_TILE], F32, name="bank")
-            for _ in range(count):
-                nc.tensor.matmul(bank[:], lhsT=zeros[:, 0:P], rhs=zeros[:], start=True, stop=True)
 
         def copy_out(on_vector, out, in_):
             if on_vector:
@@ -302,14 +294,14 @@ def tile_multiheadselfattention_pa_kernel(tc, x, W, q_out, k_out, v_out):
 
         steps = [(t, j) for t in rotated for j in range(J)]
         copies = [(t, j) for t in copied for j in range(J)]
-        warm_up(7)
-        flip_x(0)
-        flip_w(0, 0, (True, True))
-        table = square_sines(nc, fixed, phased)
-        flip_w(0, 1, (True, False))
+        flip_x(0, (False, False))
+        square_sines(nc, sines, table, phased, slice(0, 2))
+        flip_w(0, 0, (False, True))
+        flip_w(0, 1, (False, True))
         quantise_x(0)
         quantise_w(0)
-        finish_table(nc, table)
+        finish_table(nc, table, slice(0, 2))
+        square_sines(nc, sines, table, phased, slice(2, J))
         flip_x(1)
         multiply(0, 0)
         multiply(0, 1)
@@ -319,19 +311,22 @@ def tile_multiheadselfattention_pa_kernel(tc, x, W, q_out, k_out, v_out):
         multiply(0, 2)
         flip_x(3)
         rotate(0, 1)
+        finish_table(nc, table, slice(2, J))
         quantise_x(2)
         multiply(0, 3)
         done = 2
         made = 4
         for n in range(1, len(tiles)):
-            for group in range(2):
-                flip_w(n, group)
+            flip_w(n, 0)
+            flip_w(n, 1)
+            for k in range(2):
                 rotate(*steps[done])
                 done += 1
-                if n == 1 and group == 0:
-                    quantise_x(3)
-                if n > 1 and group == 0:
-                    quantise_w(n - 1)
+                if k == 0:
+                    if n == 1:
+                        quantise_x(3)
+                    else:
+                        quantise_w(n - 1)
                 multiply(*steps[made])
                 made += 1
         rotate(*steps[done])

@@ -27,7 +27,8 @@ B_BITS, J_BITS = 2, 3
 assert (1 << B_BITS, 1 << J_BITS) == (B, J)
 N_TILE = 512
 PAIRS = DH // 2
-HEADS = N_TILE // DH
+HALF = N_TILE // 2
+HEADS = HALF // DH
 QUERY, KEY, VALUE = 0, 1, 2
 
 ROUND = 1.5 * 2.0**23
@@ -108,19 +109,13 @@ def tile_multiheadselfattention_pa_kernel(tc, x, W, q_out, k_out, v_out):
         terms_pool = ctx.enter_context(tc.tile_pool(name="terms", bufs=4))
         result_pool = ctx.enter_context(tc.tile_pool(name="result", bufs=6))
         bank_pool = ctx.enter_context(tc.psum_pool(name="bank", bufs=8))
-        ctx.enter_context(tc.manual_schedule())
 
-        tiles = [
-            (QUERY, 0, q_out), (KEY, 0, k_out), (VALUE, 0, v_out),
-            (QUERY, 1, q_out), (KEY, 1, k_out), (VALUE, 1, v_out),
-        ]
-        rotated = [t for t in range(len(tiles)) if tiles[t][0] != VALUE]
-        copied = [t for t in range(len(tiles)) if tiles[t][0] == VALUE]
+        tiles = [(QUERY, 0, q_out), (VALUE, 0, v_out), (KEY, 0, k_out), (QUERY, 1, q_out), (VALUE, 1, v_out), (KEY, 1, k_out)]
 
+        x_view = x.rearrange("b (g j) c -> b g j c", j=J)
         x_pairs = [
             fixed.tile([P, 2, D], BF16, name="x_pair%d" % pair) for pair in range(J // 2)
         ]
-        x_view = x.rearrange("b (g j) c -> b g j c", j=J)
 
         def load_x(pair):
             for b in range(B):
@@ -128,25 +123,27 @@ def tile_multiheadselfattention_pa_kernel(tc, x, W, q_out, k_out, v_out):
                     out=x_pairs[pair][b:P:B], in_=x_view[b, :, 2 * pair : 2 * pair + 2, :]
                 )
 
-        w_tiles = []
+        w_halves = {}
 
-        def load_w(part, half):
-            first_row = part * H * DH + half * N_TILE
-            w_rows = w_row_pool.tile([P, 2, 2, D], BF16)
-            for g in range(2):
-                row = first_row + g * 2 * P
-                nc.sync.dma_start(
-                    out=w_rows[:, g].rearrange("p e c -> p (e c)"),
-                    in_=W[row : row + 2 * P, :].rearrange("(p e) c -> p (e c)", e=2),
-                )
-            w_tiles.append(w_rows)
+        def load_w(t):
+            part, head_half, dest = tiles[t]
+            for half in range(2):
+                w_rows = w_row_pool.tile([P, 2, D], BF16, name="w_rows%d" % half)
+                row = part * H * DH + head_half * N_TILE + half * HALF
+                rows = W[row : row + HALF, :]
+                if part == VALUE:
+                    rows = rows.rearrange("(n p) c -> p n c", n=2)
+                else:
+                    rows = rows.rearrange("(p n) c -> p n c", n=2)
+                nc.sync.dma_start(out=w_rows[:], in_=rows)
+                w_halves[t, half] = w_rows
 
         load_x(0)
-        load_w(tiles[0][0], tiles[0][1])
+        load_w(0)
         for pair in range(1, J // 2):
             load_x(pair)
-        for part, half, dest in tiles[1:]:
-            load_w(part, half)
+        for t in range(1, len(tiles)):
+            load_w(t)
 
         partition = fixed.tile([P, 1], I32)
         nc.gpsimd.iota(partition[:], pattern=[[0, 1]], base=0, channel_multiplier=1)
@@ -165,21 +162,20 @@ def tile_multiheadselfattention_pa_kernel(tc, x, W, q_out, k_out, v_out):
         grouped_x = {}
         grouped_w = {}
 
-        def copy_out(on_vector, out, in_):
+        def flip_block(words, grouped, on_vector):
+            bank = bank_pool.tile([P, PASSES, 2, P], F32, name="bank")
+            for s in range(PASSES):
+                transpose_words(nc, bank[:, s], words, identity, s)
+            in_ = bank[:].rearrange("p s u r -> p s r u")
             if on_vector:
-                nc.vector.tensor_copy(out=out, in_=in_)
+                nc.vector.tensor_copy(out=grouped.bitcast(F32), in_=in_)
             else:
-                nc.scalar.copy(out=out, in_=in_)
+                nc.scalar.copy(out=grouped.bitcast(F32), in_=in_)
 
         def flip_x(pair, on_vector=(False, False)):
             grouped = grouped_pool.tile([P, 2, PASSES, P, PACK], BF16, align_bytes=64, name="grouped_x")
             for k in range(2):
-                bank = bank_pool.tile([P, PASSES, 2, P], F32, name="bank")
-                for s in range(PASSES):
-                    transpose_words(nc, bank[:, s], x_pairs[pair][:, k, :].bitcast(F32), identity, s)
-                copy_out(
-                    on_vector[k], grouped[:, k].bitcast(F32), bank[:].rearrange("p s u r -> p s r u")
-                )
+                flip_block(x_pairs[pair][:, k, :].bitcast(F32), grouped[:, k], on_vector[k])
             grouped_x[pair] = grouped
 
         def quantise_x(pair):
@@ -190,157 +186,155 @@ def tile_multiheadselfattention_pa_kernel(tc, x, W, q_out, k_out, v_out):
                 in_=grouped_x[pair][:].rearrange("p j s n t -> p (j s n t)"),
             )
 
-        def flip_w(t, group, on_vector=(False, False)):
-            if group == 0:
+        def flip_w(t, half, on_vector=(False, False)):
+            if half == 0:
                 grouped_w[t] = grouped_pool.tile(
-                    [P, PASSES, N_TILE, PACK], BF16, align_bytes=64, name="grouped_w"
+                    [P, 2, PASSES, HALF, PACK], BF16, align_bytes=64, name="grouped_w"
                 )
-            words = grouped_w[t][:].bitcast(F32)
-            for parity in range(2):
-                bank = bank_pool.tile([P, PASSES, 2, P], F32, name="bank")
-                for s in range(PASSES):
-                    transpose_words(
-                        nc, bank[:, s], w_tiles[t][:, group, parity, :].bitcast(F32), identity, s
-                    )
-                first = P * (2 * parity + group)
-                copy_out(
-                    on_vector[parity],
-                    words[:, :, first : first + P, :],
-                    bank[:].rearrange("p s u r -> p s r u"),
+                w_codes[t] = w_mx.tile([P, 2, PASSES, HALF], U32, align_bytes=64, name="codes")
+                w_scales[t] = w_mx.tile([P, 2, PASSES, HALF], U8, align_bytes=64, name="scales")
+            for n in range(2):
+                flip_block(
+                    w_halves[t, half][:, n, :].bitcast(F32),
+                    grouped_w[t][:, half, :, n * P : (n + 1) * P, :],
+                    on_vector[n],
                 )
 
-        def quantise_w(t):
-            codes = w_mx.tile([P, PASSES, N_TILE], U32, align_bytes=64, name="codes")
-            scales = w_mx.tile([P, PASSES, N_TILE], U8, align_bytes=64, name="scales")
+        def quantise_w(t, halves=slice(0, 2)):
             nc.vector.quantize_mx(
-                out=codes[:].rearrange("p s n -> p (s n)").bitcast(FP8X4),
-                scales=scales[:].rearrange("p s n -> p (s n)"),
-                in_=grouped_w[t][:].rearrange("p s n t -> p (s n t)"),
+                out=w_codes[t][:, halves].rearrange("p g s n -> p (g s n)").bitcast(FP8X4),
+                scales=w_scales[t][:, halves].rearrange("p g s n -> p (g s n)"),
+                in_=grouped_w[t][:, halves].rearrange("p g s n t -> p (g s n t)"),
             )
-            w_codes[t] = codes
-            w_scales[t] = scales
 
         products = {}
 
-        def multiply(t, j):
-            product = bank_pool.tile([P, 2, HEADS, PAIRS], F32, name="bank")
-            for s in range(PASSES):
-                nc.tensor.matmul_mx(
-                    out=product[:].rearrange("p e h i -> p (e h i)"),
-                    lhsT=x_codes[:, j, s, :].bitcast(FP8X4),
-                    lhsT_scale=x_scales[:, j, s, :],
-                    rhs=w_codes[t][:, s, :].bitcast(FP8X4),
-                    rhs_scale=w_scales[t][:, s, :],
-                    start=(s == 0),
-                    stop=(s == PASSES - 1),
-                )
-            products[t, j] = product
+        def multiply(t, half, pair):
+            product = bank_pool.tile([P, 2, HALF], F32, name="bank")
+            for k in range(2):
+                for s in range(PASSES):
+                    nc.tensor.matmul_mx(
+                        out=product[:, k, :],
+                        lhsT=x_codes[:, 2 * pair + k, s, :].bitcast(FP8X4),
+                        lhsT_scale=x_scales[:, 2 * pair + k, s, :],
+                        rhs=w_codes[t][:, half, s, :].bitcast(FP8X4),
+                        rhs_scale=w_scales[t][:, half, s, :],
+                        start=(s == 0),
+                        stop=(s == PASSES - 1),
+                    )
+            products[t, half, pair] = product
 
         results = {}
 
-        def store_tokens(t, j):
-            size = J // 4 if t == rotated[-1] and j >= J // 2 else J // 2
-            return slice(j - j % size, j - j % size + size)
-
-        def result_of(t, j):
-            tokens = store_tokens(t, j)
-            if j == tokens.start:
-                results[t] = result_pool.tile(
-                    [P, HEADS, tokens.stop - tokens.start, DH], F32, name="result"
+        def result_of(t, half, pair):
+            group, pairs = store_group(t, half, pair)
+            if pair == pairs.start:
+                results[t, half] = result_pool.tile(
+                    [P, HEADS, 2 * (pairs.stop - pairs.start), DH], F32, name="result"
                 )
-            return results[t][:, :, j - tokens.start, :]
+            first = 2 * (pair - pairs.start)
+            return results[t, half][:, :, first : first + 2, :].rearrange("p h j d -> p j h d")
 
-        def store(t, tokens):
-            part, half, dest = tiles[t]
-            heads = slice(half * HEADS, (half + 1) * HEADS)
+        def store_group(t, half, pair):
+            size = J // 2
+            if (t, half) == LAST_HALF:
+                size = 1
+            return size, slice(pair - pair % size, pair - pair % size + size)
+
+        def finish(t, half, pair):
+            size, pairs = store_group(t, half, pair)
+            if pair != pairs.stop - 1:
+                return
+            part, head_half, dest = tiles[t]
+            first_head = 2 * HEADS * head_half + HEADS * half
+            tokens = slice(2 * pairs.start, 2 * pairs.stop)
             for b in range(B):
                 nc.sync.dma_start(
-                    out=dest[b, heads].rearrange("h (g j) d -> g h j d", j=J)[:, :, tokens, :],
-                    in_=results[t][b:P:B],
+                    out=dest[b, first_head : first_head + HEADS].rearrange("h (g j) d -> g h j d", j=J)[
+                        :, :, tokens, :
+                    ],
+                    in_=results[t, half][b:P:B],
                 )
 
-        def finish(t, j):
-            if j == store_tokens(t, j).stop - 1:
-                store(t, store_tokens(t, j))
-
-        def rotate(t, j):
-            product = products[t, j]
-            result = result_of(t, j)
-            shape = [P, 2, HEADS, PAIRS, 2]
-            terms = terms_pool.tile(shape, F32, name="terms")
+        def rotate(t, half, pair):
+            result = result_of(t, half, pair)
+            shape = [P, 4, HEADS, PAIRS, 2]
+            terms = terms_pool.tile([P, 2, 2, HEADS, DH], F32, name="terms")
+            product = products[t, half, pair][:].rearrange("p k (e h i) -> p (k e) h i", e=2, h=HEADS)
+            factors = table[:, 2 * pair : 2 * pair + 2].rearrange("p k e i r -> p (k e) i r")
             nc.vector.tensor_tensor(
-                out=terms[:],
-                in0=product[:].unsqueeze(4).to_broadcast(shape),
-                in1=table[:, j].unsqueeze(2).to_broadcast(shape),
+                out=terms[:].rearrange("p k e h (i r) -> p (k e) h i r", r=2),
+                in0=product.unsqueeze(4).to_broadcast(shape),
+                in1=factors.unsqueeze(2).to_broadcast(shape),
                 op=ALU.mult,
             )
-            adder = nc.vector if (t, j) == (rotated[-1], J - 1) else nc.gpsimd
-            adder.tensor_tensor(
-                out=result,
-                in0=terms[:, 0].rearrange("p h i r -> p h (i r)"),
-                in1=terms[:, 1].rearrange("p h i r -> p h (i r)"),
-                op=ALU.add,
-            )
-            finish(t, j)
+            adder = nc.vector if (t, half, pair) == steps[-1] else nc.gpsimd
+            adder.tensor_tensor(out=result, in0=terms[:, :, 0], in1=terms[:, :, 1], op=ALU.add)
+            finish(t, half, pair)
 
-        def copy_value(t, j):
-            product = products[t, j]
-            result = result_of(t, j)
+        def copy_value(t, half, pair):
+            result = result_of(t, half, pair)
             nc.scalar.copy(
-                out=result.rearrange("p h (i e) -> p h i e", e=2),
-                in_=product[:].rearrange("p e h i -> p h i e"),
+                out=result,
+                in_=products[t, half, pair][:].rearrange("p k (h d) -> p k h d", h=HEADS),
             )
-            finish(t, j)
+            finish(t, half, pair)
 
-        steps = [(t, j) for t in rotated for j in range(J)]
-        copies = [(t, j) for t in copied for j in range(J)]
+        steps = [(0, half, pair) for pair in range(J // 2) for half in range(2)]
+        copies = []
+        for t in range(1, len(tiles)):
+            for half in range(2):
+                for pair in range(J // 2):
+                    if tiles[t][0] == VALUE:
+                        copies.append((t, half, pair))
+                    else:
+                        steps.append((t, half, pair))
+        LAST_HALF = steps[-1][:2]
+
         flip_x(0, (False, False))
         square_sines(nc, sines, table, phased, slice(0, 2))
         flip_w(0, 0, (False, True))
-        flip_w(0, 1, (False, True))
         quantise_x(0)
-        quantise_w(0)
+        quantise_w(0, slice(0, 1))
+        flip_w(0, 1, (False, True))
         finish_table(nc, table, slice(0, 2))
         square_sines(nc, sines, table, phased, slice(2, J))
+        multiply(*steps[0])
         flip_x(1)
-        multiply(0, 0)
-        multiply(0, 1)
-        flip_x(2)
-        rotate(0, 0)
+        rotate(*steps[0])
+        quantise_w(0, slice(1, 2))
+        multiply(*steps[1])
         quantise_x(1)
-        multiply(0, 2)
-        flip_x(3)
-        rotate(0, 1)
         finish_table(nc, table, slice(2, J))
-        quantise_x(2)
-        multiply(0, 3)
-        done = 2
-        made = 4
-        for n in range(1, len(tiles)):
-            flip_w(n, 0)
-            flip_w(n, 1)
-            for k in range(2):
-                rotate(*steps[done])
-                done += 1
-                if k == 0:
-                    if n == 1:
-                        quantise_x(3)
-                    else:
-                        quantise_w(n - 1)
-                multiply(*steps[made])
-                made += 1
-        rotate(*steps[done])
-        done += 1
-        quantise_w(len(tiles) - 1)
-        copied_count = 0
-        left = len(steps) - done
-        for r in range(done, len(steps)):
-            while made < min(r + 3, len(steps)):
-                multiply(*steps[made])
-                made += 1
-            want = (r + 1 - done) * len(copies) // left
-            while copied_count < want:
-                multiply(*copies[copied_count])
-                copy_value(*copies[copied_count])
-                copied_count += 1
+        multiply(*steps[2])
+        made = 3
+        done = 1
+        copied = 0
+        ready = {0}
+        ready_x = 2
+        runs = {3: 2, 4: 1, 8: 3, 11: 4, 15: 5}
+        x_runs = {1: 2, 2: 3}
+        for r in range(1, len(steps)):
+            if r in x_runs:
+                flip_x(x_runs[r])
+            if r in runs:
+                flip_w(runs[r], 0)
+                flip_w(runs[r], 1)
             rotate(*steps[r])
+            if r - 1 in x_runs:
+                quantise_x(x_runs[r - 1])
+                ready_x = x_runs[r - 1] + 1
+            if r - 3 in runs:
+                quantise_w(runs[r - 3])
+                ready.add(runs[r - 3])
+            while made < min(r + 1 + 3, len(steps)):
+                t, half, pair = steps[made]
+                if t not in ready or pair >= ready_x:
+                    break
+                multiply(t, half, pair)
+                made += 1
+            want = (r + 1 - 6) * len(copies) // (len(steps) - 6 - 6)
+            while copied < min(want, len(copies)) and copies[copied][0] in ready:
+                multiply(*copies[copied])
+                copy_value(*copies[copied])
+                copied += 1

@@ -237,8 +237,10 @@ def tile_multiheadselfattention_pa_kernel(tc, x, W, q_out, k_out, v_out):
 
         def store_group(t, half, pair):
             size = J // 2
+            if t == 0:
+                size = 2
             if (t, half) == LAST_HALF:
-                size = 1
+                size = 2
             return size, slice(pair - pair % size, pair - pair % size + size)
 
         def finish(t, half, pair):
@@ -312,7 +314,7 @@ def tile_multiheadselfattention_pa_kernel(tc, x, W, q_out, k_out, v_out):
         copied = 0
         ready = {0}
         ready_x = 2
-        runs = {3: 2, 4: 1, 8: 3, 11: 4, 15: 5}
+        runs = {3: 2, 4: 1, 10: 3, 11: 4, 17: 5}
         x_runs = {1: 2, 2: 3}
         for r in range(1, len(steps)):
             if r in x_runs:
@@ -324,16 +326,16 @@ def tile_multiheadselfattention_pa_kernel(tc, x, W, q_out, k_out, v_out):
             if r - 1 in x_runs:
                 quantise_x(x_runs[r - 1])
                 ready_x = x_runs[r - 1] + 1
-            if r - 3 in runs:
-                quantise_w(runs[r - 3])
-                ready.add(runs[r - 3])
+            if r - 2 in runs:
+                quantise_w(runs[r - 2])
+                ready.add(runs[r - 2])
             while made < min(r + 1 + 3, len(steps)):
                 t, half, pair = steps[made]
                 if t not in ready or pair >= ready_x:
                     break
                 multiply(t, half, pair)
                 made += 1
-            want = (r + 1 - 6) * len(copies) // (len(steps) - 6 - 6)
+            want = (r + 1 - 5) * len(copies) // (len(steps) - 6 - 5)
             while copied < min(want, len(copies)) and copies[copied][0] in ready:
                 multiply(*copies[copied])
                 copy_value(*copies[copied])

@@ -109,6 +109,7 @@ def tile_multiheadselfattention_pa_kernel(tc, x, W, q_out, k_out, v_out):
         terms_pool = ctx.enter_context(tc.tile_pool(name="terms", bufs=4))
         result_pool = ctx.enter_context(tc.tile_pool(name="result", bufs=6))
         bank_pool = ctx.enter_context(tc.psum_pool(name="bank", bufs=8))
+        ctx.enter_context(tc.manual_schedule(engines={mybir.EngineType.PE}))
 
         tiles = [(QUERY, 0, q_out), (VALUE, 0, v_out), (KEY, 0, k_out), (QUERY, 1, q_out), (VALUE, 1, v_out), (KEY, 1, k_out)]
 
@@ -300,42 +301,46 @@ def tile_multiheadselfattention_pa_kernel(tc, x, W, q_out, k_out, v_out):
         quantise_w(0, slice(0, 1))
         flip_w(0, 1, (False, True))
         finish_table(nc, table, slice(0, 2))
-        square_sines(nc, sines, table, phased, slice(2, J))
-        multiply(*steps[0])
         flip_x(1)
+        multiply(*steps[0])
+        square_sines(nc, sines, table, phased, slice(2, J))
         rotate(*steps[0])
         quantise_w(0, slice(1, 2))
         multiply(*steps[1])
+        flip_x(2)
         quantise_x(1)
+        rotate(*steps[1])
         finish_table(nc, table, slice(2, J))
         multiply(*steps[2])
-        made = 3
-        done = 1
+        multiply(*steps[3])
+        flip_x(3)
+        rotate(*steps[2])
+        quantise_x(2)
+        multiply(*steps[4])
+        multiply(*steps[5])
+        rotate(*steps[3])
+        quantise_x(3)
+        made = 6
+        done = 4
         copied = 0
         ready = {0}
-        ready_x = 2
-        runs = {3: 2, 4: 1, 10: 3, 11: 4, 17: 5}
-        x_runs = {1: 2, 2: 3}
-        for r in range(1, len(steps)):
-            if r in x_runs:
-                flip_x(x_runs[r])
-            if r in runs:
-                flip_w(runs[r], 0)
-                flip_w(runs[r], 1)
+        runs = {4: [2, 1], 9: [3, 4], 16: [5]}
+        quants = {6: 2, 7: 1, 12: 3, 14: 4, 19: 5}
+        for r in range(done, len(steps)):
+            for t in runs.get(r, []):
+                flip_w(t, 0)
+                flip_w(t, 1)
             rotate(*steps[r])
-            if r - 1 in x_runs:
-                quantise_x(x_runs[r - 1])
-                ready_x = x_runs[r - 1] + 1
-            if r - 2 in runs:
-                quantise_w(runs[r - 2])
-                ready.add(runs[r - 2])
+            if r in quants:
+                quantise_w(quants[r])
+                ready.add(quants[r])
             while made < min(r + 1 + 3, len(steps)):
                 t, half, pair = steps[made]
-                if t not in ready or pair >= ready_x:
+                if t not in ready:
                     break
                 multiply(t, half, pair)
                 made += 1
-            want = (r + 1 - 5) * len(copies) // (len(steps) - 6 - 5)
+            want = (r + 1 - 8) * len(copies) // (len(steps) - 5 - 8)
             while copied < min(want, len(copies)) and copies[copied][0] in ready:
                 multiply(*copies[copied])
                 copy_value(*copies[copied])

@@ -227,14 +227,19 @@ def tile_multiheadselfattention_pa_kernel(tc, x, W, q_out, k_out, v_out):
 
         results = {}
 
-        def result_of(t, half, pair):
-            group, pairs = store_group(t, half, pair)
+        terms_of = {}
+
+        def result_start(t, half, pair):
+            size, pairs = store_group(t, half, pair)
             if pair == pairs.start:
                 results[t, half] = result_pool.tile(
                     [P, HEADS, 2 * (pairs.stop - pairs.start), DH], F32, name="result"
                 )
-            first = 2 * (pair - pairs.start)
-            return results[t, half][:, :, first : first + 2, :].rearrange("p h j d -> p j h d")
+
+        def result_of(t, half, pair, width):
+            size, pairs = store_group(t, half, pair)
+            last = 2 * (pair - pairs.start) + 2
+            return results[t, half][:, :, last - width : last, :].rearrange("p h j d -> p j h d")
 
         def store_group(t, half, pair):
             size = J // 2
@@ -260,25 +265,35 @@ def tile_multiheadselfattention_pa_kernel(tc, x, W, q_out, k_out, v_out):
                 )
 
         def rotate(t, half, pair):
-            result = result_of(t, half, pair)
+            width = 4 if t > 0 else 2
+            first = 2 * (pair % 2) if width == 4 else 0
+            if first == 0:
+                terms_of[0] = terms_pool.tile(
+                    [P, width, 2, HEADS, DH], F32, name="terms%d" % width, bufs=3
+                )
+            terms = terms_of[0]
             shape = [P, 4, HEADS, PAIRS, 2]
-            terms = terms_pool.tile([P, 2, 2, HEADS, DH], F32, name="terms")
             product = products[t, half, pair][:].rearrange("p k (e h i) -> p (k e) h i", e=2, h=HEADS)
             factors = table[:, 2 * pair : 2 * pair + 2].rearrange("p k e i r -> p (k e) i r")
             nc.vector.tensor_tensor(
-                out=terms[:].rearrange("p k e h (i r) -> p (k e) h i r", r=2),
+                out=terms[:, first : first + 2].rearrange("p k e h (i r) -> p (k e) h i r", r=2),
                 in0=product.unsqueeze(4).to_broadcast(shape),
                 in1=factors.unsqueeze(2).to_broadcast(shape),
                 op=ALU.mult,
             )
+            result_start(t, half, pair)
+            if first + 2 < width:
+                return
             adder = nc.vector if (t, half, pair) == steps[-1] else nc.gpsimd
-            adder.tensor_tensor(out=result, in0=terms[:, :, 0], in1=terms[:, :, 1], op=ALU.add)
+            adder.tensor_tensor(
+                out=result_of(t, half, pair, width), in0=terms[:, :, 0], in1=terms[:, :, 1], op=ALU.add
+            )
             finish(t, half, pair)
 
         def copy_value(t, half, pair):
-            result = result_of(t, half, pair)
+            result_start(t, half, pair)
             nc.scalar.copy(
-                out=result,
+                out=result_of(t, half, pair, 2),
                 in_=products[t, half, pair][:].rearrange("p k (h d) -> p k h d", h=HEADS),
             )
             finish(t, half, pair)

@@ -76,8 +76,11 @@ def build_angles(nc, pool, partition, token):
     return phased
 
 
-def square_sines(nc, sines, table, phased, tokens):
+def make_sines(nc, sines, phased, tokens):
     nc.scalar.activation(out=sines[:, tokens], in_=phased[:, tokens], func=ACT.Sin, scale=0.5)
+
+
+def square_sines(nc, sines, table, tokens):
     for source in range(2):
         nc.scalar.activation(
             out=table[:, tokens, source],
@@ -86,8 +89,8 @@ def square_sines(nc, sines, table, phased, tokens):
         )
 
 
-def finish_table(nc, table, tokens):
-    nc.vector.tensor_scalar(
+def finish_table(engine, table, tokens):
+    engine.tensor_scalar(
         out=table[:, tokens], in0=table[:, tokens], scalar1=-2.0, scalar2=1.0, op0=ALU.mult, op1=ALU.add
     )
 
@@ -114,45 +117,49 @@ def tile_multiheadselfattention_pa_kernel(tc, x, W, q_out, k_out, v_out):
         tiles = [(QUERY, 0, q_out), (VALUE, 0, v_out), (KEY, 0, k_out), (QUERY, 1, q_out), (VALUE, 1, v_out), (KEY, 1, k_out)]
 
         x_view = x.rearrange("b (g j) c -> b g j c", j=J)
-        x_pairs = [
-            fixed.tile([P, 2, D], BF16, name="x_pair%d" % pair) for pair in range(J // 2)
-        ]
+        x_rows = {}
 
-        def load_x(pair):
+        def load_x(first, count):
+            rows = fixed.tile([P, count, D], BF16, name="x_rows%d" % first)
             for b in range(B):
-                nc.sync.dma_start(
-                    out=x_pairs[pair][b:P:B], in_=x_view[b, :, 2 * pair : 2 * pair + 2, :]
-                )
+                nc.sync.dma_start(out=rows[b:P:B], in_=x_view[b, :, first : first + count, :])
+            for k in range(count):
+                x_rows[first + k] = rows[:, k, :]
 
         w_halves = {}
 
-        def load_w(t):
+        def load_w(t, half):
             part, head_half, dest = tiles[t]
-            for half in range(2):
-                w_rows = w_row_pool.tile([P, 2, D], BF16, name="w_rows%d" % half)
-                row = part * H * DH + head_half * N_TILE + half * HALF
-                rows = W[row : row + HALF, :]
-                if part == VALUE:
-                    rows = rows.rearrange("(n p) c -> p n c", n=2)
-                else:
-                    rows = rows.rearrange("(p n) c -> p n c", n=2)
-                nc.sync.dma_start(out=w_rows[:], in_=rows)
-                w_halves[t, half] = w_rows
+            w_rows = w_row_pool.tile([P, 2, D], BF16, name="w_rows%d" % half)
+            row = part * H * DH + head_half * N_TILE + half * HALF
+            rows = W[row : row + HALF, :]
+            if part == VALUE:
+                rows = rows.rearrange("(n p) c -> p n c", n=2)
+            else:
+                rows = rows.rearrange("(p n) c -> p n c", n=2)
+            nc.sync.dma_start(out=w_rows[:], in_=rows)
+            w_halves[t, half] = w_rows
 
-        load_x(0)
-        load_w(0)
+        load_x(0, 1)
+        load_w(0, 0)
+        load_x(1, 1)
+        load_w(0, 1)
         for pair in range(1, J // 2):
-            load_x(pair)
+            load_x(2 * pair, 2)
         for t in range(1, len(tiles)):
-            load_w(t)
+            for half in range(2):
+                load_w(t, half)
 
         partition = fixed.tile([P, 1], I32)
         nc.gpsimd.iota(partition[:], pattern=[[0, 1]], base=0, channel_multiplier=1)
         token = fixed.tile([P, J], I32)
         nc.gpsimd.iota(token[:], pattern=[[1, J]], base=0, channel_multiplier=0)
+        zero = fixed.tile([P, 1], F32)
+        nc.gpsimd.memset(zero[:], 0.0)
+        warm = fixed.tile([P, 1], F32)
+        nc.scalar.activation(out=warm[:], in_=zero[:], func=ACT.Sin)
         identity = fixed.tile([P, P], F32)
         make_identity(nc, identity[:])
-        phased = build_angles(nc, fixed, partition, token)
         sines = fixed.tile([P, J, 3, PAIRS], F32)
         table = fixed.tile([P, J, 2, PAIRS, 2], F32)
 
@@ -173,18 +180,20 @@ def tile_multiheadselfattention_pa_kernel(tc, x, W, q_out, k_out, v_out):
             else:
                 nc.scalar.copy(out=grouped.bitcast(F32), in_=in_)
 
-        def flip_x(pair, on_vector=(False, False)):
-            grouped = grouped_pool.tile([P, 2, PASSES, P, PACK], BF16, align_bytes=64, name="grouped_x")
-            for k in range(2):
-                flip_block(x_pairs[pair][:, k, :].bitcast(F32), grouped[:, k], on_vector[k])
-            grouped_x[pair] = grouped
+        def flip_x(first, count):
+            grouped = grouped_pool.tile(
+                [P, count, PASSES, P, PACK], BF16, align_bytes=64, name="grouped_x%d" % count
+            )
+            for k in range(count):
+                flip_block(x_rows[first + k].bitcast(F32), grouped[:, k], False)
+            grouped_x[first] = grouped
 
-        def quantise_x(pair):
-            pair_tokens = slice(2 * pair, 2 * pair + 2)
+        def quantise_x(first, count):
+            tokens = slice(first, first + count)
             nc.vector.quantize_mx(
-                out=x_codes[:, pair_tokens].rearrange("p j s n -> p (j s n)").bitcast(FP8X4),
-                scales=x_scales[:, pair_tokens].rearrange("p j s n -> p (j s n)"),
-                in_=grouped_x[pair][:].rearrange("p j s n t -> p (j s n t)"),
+                out=x_codes[:, tokens].rearrange("p j s n -> p (j s n)").bitcast(FP8X4),
+                scales=x_scales[:, tokens].rearrange("p j s n -> p (j s n)"),
+                in_=grouped_x[first][:].rearrange("p j s n t -> p (j s n t)"),
             )
 
         def flip_w(t, half, on_vector=(False, False)):
@@ -269,7 +278,7 @@ def tile_multiheadselfattention_pa_kernel(tc, x, W, q_out, k_out, v_out):
             first = 2 * (pair % 2) if width == 4 else 0
             if first == 0:
                 terms_of[0] = terms_pool.tile(
-                    [P, width, 2, HEADS, DH], F32, name="terms%d" % width, bufs=3
+                    [P, width, 2, HEADS, DH], F32, name="terms%d" % width, bufs=3 if width == 4 else 2
                 )
             terms = terms_of[0]
             shape = [P, 4, HEADS, PAIRS, 2]
@@ -309,32 +318,38 @@ def tile_multiheadselfattention_pa_kernel(tc, x, W, q_out, k_out, v_out):
                         steps.append((t, half, pair))
         LAST_HALF = steps[-1][:2]
 
-        flip_x(0, (False, False))
-        square_sines(nc, sines, table, phased, slice(0, 2))
-        flip_w(0, 0, (False, True))
-        quantise_x(0)
-        quantise_w(0, slice(0, 1))
-        flip_w(0, 1, (False, True))
-        finish_table(nc, table, slice(0, 2))
-        flip_x(1)
-        multiply(*steps[0])
-        square_sines(nc, sines, table, phased, slice(2, J))
-        rotate(*steps[0])
-        quantise_w(0, slice(1, 2))
-        multiply(*steps[1])
-        flip_x(2)
-        quantise_x(1)
-        rotate(*steps[1])
-        finish_table(nc, table, slice(2, J))
-        multiply(*steps[2])
-        multiply(*steps[3])
-        flip_x(3)
-        rotate(*steps[2])
-        quantise_x(2)
-        multiply(*steps[4])
-        multiply(*steps[5])
-        rotate(*steps[3])
-        quantise_x(3)
+        with tc.manual_schedule(engines={mybir.EngineType.DVE, mybir.EngineType.Activation}):
+            phased = build_angles(nc, fixed, partition, token)
+            flip_x(0, 1)
+            quantise_x(0, 1)
+            flip_w(0, 0, (False, True))
+            make_sines(nc, sines, phased, slice(0, 2))
+            square_sines(nc, sines, table, slice(0, 2))
+            flip_x(1, 1)
+            quantise_w(0, slice(0, 1))
+            finish_table(nc.vector, table, slice(0, 2))
+            quantise_x(1, 1)
+            make_sines(nc, sines, phased, slice(2, J))
+            flip_w(0, 1, (False, True))
+            multiply(*steps[0])
+            quantise_w(0, slice(1, 2))
+            rotate(*steps[0])
+            square_sines(nc, sines, table, slice(2, J))
+            flip_x(2, 2)
+            multiply(*steps[1])
+            quantise_x(2, 2)
+            rotate(*steps[1])
+            finish_table(nc.gpsimd, table, slice(2, J))
+            flip_x(4, 2)
+            multiply(*steps[2])
+            multiply(*steps[3])
+            rotate(*steps[2])
+            quantise_x(4, 2)
+            flip_x(6, 2)
+            multiply(*steps[4])
+            multiply(*steps[5])
+            rotate(*steps[3])
+            quantise_x(6, 2)
         made = 6
         done = 4
         copied = 0

@@ -106,13 +106,18 @@ def tile_multiheadselfattention_pa_kernel(tc, x, W, q_out, k_out, v_out):
     nc = tc.nc
     with ExitStack() as ctx:
         fixed = ctx.enter_context(tc.tile_pool(name="fixed", bufs=1))
-        w_row_pool = ctx.enter_context(tc.tile_pool(name="w_rows", bufs=6))
+        w_row_pool = ctx.enter_context(tc.tile_pool(name="w_rows", bufs=4))
+        word_pool = ctx.enter_context(tc.tile_pool(name="words", bufs=3))
         grouped_pool = ctx.enter_context(tc.tile_pool(name="grouped", bufs=3))
         w_mx = ctx.enter_context(tc.tile_pool(name="w_mx", bufs=6))
         terms_pool = ctx.enter_context(tc.tile_pool(name="terms", bufs=4))
         result_pool = ctx.enter_context(tc.tile_pool(name="result", bufs=6))
         bank_pool = ctx.enter_context(tc.psum_pool(name="bank", bufs=8))
-        ctx.enter_context(tc.manual_schedule(engines={mybir.EngineType.PE}))
+        ctx.enter_context(
+            tc.manual_schedule(
+                engines={mybir.EngineType.PE, mybir.EngineType.Activation, mybir.EngineType.DVE}
+            )
+        )
 
         tiles = [(QUERY, 0, q_out), (VALUE, 0, v_out), (KEY, 0, k_out), (QUERY, 1, q_out), (VALUE, 1, v_out), (KEY, 1, k_out)]
 
@@ -170,10 +175,14 @@ def tile_multiheadselfattention_pa_kernel(tc, x, W, q_out, k_out, v_out):
         grouped_x = {}
         grouped_w = {}
 
-        def flip_block(words, grouped, on_vector):
-            bank = bank_pool.tile([P, PASSES, 2, P], F32, name="bank")
+        def flip_block(words, grouped, on_vector, ordered=False):
+            bank = bank_pool.tile([P, PASSES, 2, P], F32, name="bank", bufs=4)
             for s in range(PASSES):
-                transpose_words(nc, bank[:, s], words, identity, s)
+                if ordered:
+                    for u in range(2):
+                        nc.tensor.transpose(bank[:, s, u, :], words[:, s, u, :], identity[:])
+                else:
+                    transpose_words(nc, bank[:, s], words, identity, s)
             in_ = bank[:].rearrange("p s u r -> p s r u")
             if on_vector:
                 nc.vector.tensor_copy(out=grouped.bitcast(F32), in_=in_)
@@ -196,6 +205,19 @@ def tile_multiheadselfattention_pa_kernel(tc, x, W, q_out, k_out, v_out):
                 in_=grouped_x[first][:].rearrange("p j s n t -> p (j s n t)"),
             )
 
+        words_of = {}
+
+        def order_words(t, half):
+            words = word_pool.tile([P, 2, PASSES, 2, P], F32, name="words")
+            nc.scalar.copy(
+                out=words[:].rearrange("p n s u q -> p (n s) u q"),
+                in_=w_halves[t, half][:]
+                .rearrange("p n c -> p (n c)")
+                .bitcast(F32)
+                .rearrange("p (m q u) -> p m u q", q=P, u=2),
+            )
+            words_of[t, half] = words
+
         def flip_w(t, half, on_vector=(False, False)):
             if half == 0:
                 grouped_w[t] = grouped_pool.tile(
@@ -204,10 +226,12 @@ def tile_multiheadselfattention_pa_kernel(tc, x, W, q_out, k_out, v_out):
                 w_codes[t] = w_mx.tile([P, 2, PASSES, HALF], U32, align_bytes=64, name="codes")
                 w_scales[t] = w_mx.tile([P, 2, PASSES, HALF], U8, align_bytes=64, name="scales")
             for n in range(2):
+                ordered = (t, half) in words_of
                 flip_block(
-                    w_halves[t, half][:, n, :].bitcast(F32),
+                    words_of[t, half][:, n] if ordered else w_halves[t, half][:, n, :].bitcast(F32),
                     grouped_w[t][:, half, :, n * P : (n + 1) * P, :],
                     on_vector[n],
+                    ordered,
                 )
 
         def quantise_w(t, halves=slice(0, 2)):
@@ -220,7 +244,10 @@ def tile_multiheadselfattention_pa_kernel(tc, x, W, q_out, k_out, v_out):
         products = {}
 
         def multiply(t, half, pair):
-            product = bank_pool.tile([P, 2, HALF], F32, name="bank")
+            rotated = tiles[t][0] != VALUE
+            product = bank_pool.tile(
+                [P, 2, HALF], F32, name="product" if rotated else "bank", bufs=4 if rotated else 4
+            )
             for k in range(2):
                 for s in range(PASSES):
                     nc.tensor.matmul_mx(
@@ -318,49 +345,51 @@ def tile_multiheadselfattention_pa_kernel(tc, x, W, q_out, k_out, v_out):
                         steps.append((t, half, pair))
         LAST_HALF = steps[-1][:2]
 
-        with tc.manual_schedule(engines={mybir.EngineType.DVE, mybir.EngineType.Activation}):
-            phased = build_angles(nc, fixed, partition, token)
-            flip_x(0, 1)
-            quantise_x(0, 1)
-            flip_w(0, 0, (False, True))
-            make_sines(nc, sines, phased, slice(0, 2))
-            square_sines(nc, sines, table, slice(0, 2))
-            flip_x(1, 1)
-            quantise_w(0, slice(0, 1))
-            finish_table(nc.vector, table, slice(0, 2))
-            quantise_x(1, 1)
-            make_sines(nc, sines, phased, slice(2, J))
-            flip_w(0, 1, (False, True))
-            multiply(*steps[0])
-            quantise_w(0, slice(1, 2))
-            rotate(*steps[0])
-            square_sines(nc, sines, table, slice(2, J))
-            flip_x(2, 2)
-            multiply(*steps[1])
-            quantise_x(2, 2)
-            rotate(*steps[1])
-            finish_table(nc.gpsimd, table, slice(2, J))
-            flip_x(4, 2)
-            multiply(*steps[2])
-            multiply(*steps[3])
-            rotate(*steps[2])
-            quantise_x(4, 2)
-            flip_x(6, 2)
-            multiply(*steps[4])
-            multiply(*steps[5])
-            rotate(*steps[3])
-            quantise_x(6, 2)
+        phased = build_angles(nc, fixed, partition, token)
+        flip_x(0, 1)
+        quantise_x(0, 1)
+        flip_w(0, 0, (False, True))
+        make_sines(nc, sines, phased, slice(0, 2))
+        square_sines(nc, sines, table, slice(0, 2))
+        flip_x(1, 1)
+        quantise_w(0, slice(0, 1))
+        finish_table(nc.vector, table, slice(0, 2))
+        quantise_x(1, 1)
+        make_sines(nc, sines, phased, slice(2, J))
+        flip_w(0, 1, (False, True))
+        multiply(*steps[0])
+        quantise_w(0, slice(1, 2))
+        rotate(*steps[0])
+        square_sines(nc, sines, table, slice(2, J))
+        flip_x(2, 2)
+        multiply(*steps[1])
+        quantise_x(2, 2)
+        rotate(*steps[1])
+        finish_table(nc.vector, table, slice(2, J))
+        flip_x(4, 2)
+        multiply(*steps[2])
+        multiply(*steps[3])
+        rotate(*steps[2])
+        quantise_x(4, 2)
+        flip_x(6, 2)
+        flip_w(2, 0)
+        multiply(*steps[4])
+        multiply(*steps[5])
+        rotate(*steps[3])
+        quantise_x(6, 2)
         made = 6
         done = 4
         copied = 0
         ready = {0}
-        runs = {4: [2, 1], 9: [3, 4], 16: [5]}
-        quants = {6: 2, 7: 1, 12: 3, 14: 4, 19: 5}
+        flips = {4: [(2, 1)], 7: [(3, 0)], 8: [(3, 1)], 11: [(1, 0)], 12: [(1, 1)], 14: [(4, 0)], 15: [(4, 1)], 17: [(5, 0)], 18: [(5, 1)]}
+        quants = {5: 2, 11: 3, 15: 1, 19: 4, 21: 5}
         for r in range(done, len(steps)):
-            for t in runs.get(r, []):
-                flip_w(t, 0)
-                flip_w(t, 1)
+            for t, half in flips.get(r, []):
+                flip_w(t, half)
             rotate(*steps[r])
+            for t, half in flips.get(r + 2, []):
+                if t in [1, 3, 4, 5]:
+                    order_words(t, half)
             if r in quants:
                 quantise_w(quants[r])
                 ready.add(quants[r])
@@ -370,7 +399,7 @@ def tile_multiheadselfattention_pa_kernel(tc, x, W, q_out, k_out, v_out):
                     break
                 multiply(t, half, pair)
                 made += 1
-            want = (r + 1 - 8) * len(copies) // (len(steps) - 5 - 8)
+            want = (r + 1 - 15) * len(copies) // (len(steps) - 5 - 15)
             while copied < min(want, len(copies)) and copies[copied][0] in ready:
                 multiply(*copies[copied])
                 copy_value(*copies[copied])

@@ -305,7 +305,7 @@ def tile_multiheadselfattention_pa_kernel(tc, x, W, q_out, k_out, v_out):
             first = 2 * (pair % 2) if width == 4 else 0
             if first == 0:
                 terms_of[0] = terms_pool.tile(
-                    [P, width, 2, HEADS, DH], F32, name="terms%d" % width, bufs=3 if width == 4 else 2
+                    [P, width, 2, HEADS, DH], F32, name="terms%d" % width, bufs=3
                 )
             terms = terms_of[0]
             shape = [P, 4, HEADS, PAIRS, 2]
@@ -364,8 +364,8 @@ def tile_multiheadselfattention_pa_kernel(tc, x, W, q_out, k_out, v_out):
         flip_x(2, 2)
         multiply(*steps[1])
         quantise_x(2, 2)
-        rotate(*steps[1])
         finish_table(nc.vector, table, slice(2, J))
+        rotate(*steps[1])
         flip_x(4, 2)
         multiply(*steps[2])
         multiply(*steps[3])
@@ -373,6 +373,7 @@ def tile_multiheadselfattention_pa_kernel(tc, x, W, q_out, k_out, v_out):
         quantise_x(4, 2)
         flip_x(6, 2)
         flip_w(2, 0)
+        flip_w(2, 1)
         multiply(*steps[4])
         multiply(*steps[5])
         rotate(*steps[3])
@@ -381,14 +382,14 @@ def tile_multiheadselfattention_pa_kernel(tc, x, W, q_out, k_out, v_out):
         done = 4
         copied = 0
         ready = {0}
-        flips = {4: [(2, 1)], 7: [(3, 0)], 8: [(3, 1)], 11: [(1, 0)], 12: [(1, 1)], 14: [(4, 0)], 15: [(4, 1)], 17: [(5, 0)], 18: [(5, 1)]}
-        quants = {5: 2, 11: 3, 15: 1, 19: 4, 21: 5}
+        flips = {5: [(1, 0)], 6: [(1, 1)], 8: [(3, 0)], 9: [(3, 1)], 12: [(4, 0)], 13: [(4, 1)], 17: [(5, 0)], 18: [(5, 1)]}
+        quants = {4: 2, 9: 1, 11: 3, 15: 4, 21: 5}
         for r in range(done, len(steps)):
             for t, half in flips.get(r, []):
                 flip_w(t, half)
             rotate(*steps[r])
-            for t, half in flips.get(r + 2, []):
-                if t in [1, 3, 4, 5]:
+            for t, half in flips.get(r + 3, []):
+                if t in [4, 5]:
                     order_words(t, half)
             if r in quants:
                 quantise_w(quants[r])
@@ -399,7 +400,7 @@ def tile_multiheadselfattention_pa_kernel(tc, x, W, q_out, k_out, v_out):
                     break
                 multiply(t, half, pair)
                 made += 1
-            want = (r + 1 - 15) * len(copies) // (len(steps) - 5 - 15)
+            want = (r + 1 - 9) * len(copies) // (len(steps) - 9 - 9)
             while copied < min(want, len(copies)) and copies[copied][0] in ready:
                 multiply(*copies[copied])
                 copy_value(*copies[copied])

from contextlib import ExitStack
import math

import concourse.mybir as mybir
from concourse.masks import make_identity

F32 = mybir.dt.float32
BF16 = mybir.dt.bfloat16
I32 = mybir.dt.int32
U32 = mybir.dt.uint32
U8 = mybir.dt.uint8
FP8X4 = mybir.dt.float8_e4m3fn_x4
ALU = mybir.AluOpType
ACT = mybir.ActivationFunctionType

B, L, D, H, DH = 4, 256, 1024, 16, 64
THETA = 100000.0
FLOPS = 2 * B * L * D * 3 * H * DH

P = 128
PACK = 4
PASSES = D // (P * PACK)
WORDS = D // 2
CHUNKS = WORDS // P
J = B * L // P
B_BITS, J_BITS = 2, 3
assert (1 << B_BITS, 1 << J_BITS) == (B, J)
N_TILE = 512
PAIRS = DH // 2
HALF = N_TILE // 2
HEADS = HALF // DH
QUERY, KEY, VALUE = 0, 1, 2

ROUND = 1.5 * 2.0**23
TURN_HI = 6.28125
TURN_LO = 2.0 * math.pi - TURN_HI


def build_angles(nc, pool, partition, token):
    first = pool.tile([P, 1], I32)
    nc.vector.tensor_scalar(
        out=first[:],
        in0=partition[:],
        scalar1=B_BITS,
        scalar2=J_BITS,
        op0=ALU.logical_shift_right,
        op1=ALU.logical_shift_left,
    )
    angle = pool.tile([P, J, PAIRS], F32)
    nc.vector.tensor_scalar_add(out=angle[:, :, 0], in0=token[:], scalar1=first[:, 0:1])
    have = 1
    while have < PAIRS:
        nc.vector.tensor_scalar_mul(
            out=angle[:, :, have : 2 * have],
            in0=angle[:, :, 0:have],
            scalar1=THETA ** (-2.0 * have / DH),
        )
        have *= 2

    turns = pool.tile([P, J, PAIRS], F32)
    nc.vector.tensor_scalar(
        out=turns[:], in0=angle[:], scalar1=0.5 / math.pi, scalar2=ROUND, op0=ALU.mult, op1=ALU.add
    )
    nc.vector.tensor_scalar_add(out=turns[:], in0=turns[:], scalar1=-ROUND)
    nc.vector.scalar_tensor_tensor(
        out=angle[:], in0=turns[:], scalar=-TURN_HI, in1=angle[:], op0=ALU.mult, op1=ALU.add
    )
    phased = pool.tile([P, J, 3, PAIRS], F32)
    nc.vector.scalar_tensor_tensor(
        out=phased[:, :, 1, :], in0=turns[:], scalar=-TURN_LO, in1=angle[:], op0=ALU.mult, op1=ALU.add
    )
    for m in (0, 2):
        nc.vector.tensor_scalar_add(
            out=phased[:, :, m, :], in0=phased[:, :, 1, :], scalar1=(1 - m) * 0.5 * math.pi
        )
    return phased


def make_sines(nc, sines, phased, tokens):
    nc.scalar.activation(out=sines[:, tokens], in_=phased[:, tokens], func=ACT.Sin, scale=0.5)


def square_sines(nc, sines, table, tokens):
    for source in range(2):
        nc.scalar.activation(
            out=table[:, tokens, source],
            in_=sines[:, tokens, 1 - source : 3 - source, :].rearrange("p j r i -> p j i r"),
            func=ACT.Square,
        )


def finish_table(engine, table, tokens):
    engine.tensor_scalar(
        out=table[:, tokens], in0=table[:, tokens], scalar1=-2.0, scalar2=1.0, op0=ALU.mult, op1=ALU.add
    )


def transpose_words(nc, bank, words, identity, s):
    for u in range(2):
        nc.tensor.transpose(
            bank[:, u, :], words[:, 2 * P * s + u : 2 * P * (s + 1) : 2], identity[:]
        )


def tile_multiheadselfattention_pa_kernel(tc, x, W, q_out, k_out, v_out):
    nc = tc.nc
    with ExitStack() as ctx:
        fixed = ctx.enter_context(tc.tile_pool(name="fixed", bufs=1))
        w_row_pool = ctx.enter_context(tc.tile_pool(name="w_rows", bufs=4))
        word_pool = ctx.enter_context(tc.tile_pool(name="words", bufs=3))
        grouped_pool = ctx.enter_context(tc.tile_pool(name="grouped", bufs=3))
        w_mx = ctx.enter_context(tc.tile_pool(name="w_mx", bufs=6))
        terms_pool = ctx.enter_context(tc.tile_pool(name="terms", bufs=4))
        result_pool = ctx.enter_context(tc.tile_pool(name="result", bufs=6))
        bank_pool = ctx.enter_context(tc.psum_pool(name="bank", bufs=8))
        ctx.enter_context(
            tc.manual_schedule(
                engines={mybir.EngineType.PE, mybir.EngineType.Activation, mybir.EngineType.DVE}
            )
        )

        tiles = [(QUERY, 0, q_out), (VALUE, 0, v_out), (KEY, 0, k_out), (QUERY, 1, q_out), (VALUE, 1, v_out), (KEY, 1, k_out)]

        x_view = x.rearrange("b (g j) c -> b g j c", j=J)
        x_rows = {}

        def load_x(first, count):
            rows = fixed.tile([P, count, D], BF16, name="x_rows%d" % first)
            for b in range(B):
                nc.sync.dma_start(out=rows[b:P:B], in_=x_view[b, :, first : first + count, :])
            for k in range(count):
                x_rows[first + k] = rows[:, k, :]

        w_halves = {}

        def load_w(t, half):
            part, head_half, dest = tiles[t]
            w_rows = w_row_pool.tile([P, 2, D], BF16, name="w_rows%d" % half)
            row = part * H * DH + head_half * N_TILE + half * HALF
            rows = W[row : row + HALF, :]
            if part == VALUE:
                rows = rows.rearrange("(n p) c -> p n c", n=2)
            else:
                rows = rows.rearrange("(p n) c -> p n c", n=2)
            nc.sync.dma_start(out=w_rows[:], in_=rows)
            w_halves[t, half] = w_rows

        load_x(0, 1)
        load_w(0, 0)
        load_x(1, 1)
        load_w(0, 1)
        for pair in range(1, J // 2):
            load_x(2 * pair, 2)
        for t in range(1, len(tiles)):
            for half in range(2):
                load_w(t, half)

        partition = fixed.tile([P, 1], I32)
        nc.gpsimd.iota(partition[:], pattern=[[0, 1]], base=0, channel_multiplier=1)
        token = fixed.tile([P, J], I32)
        nc.gpsimd.iota(token[:], pattern=[[1, J]], base=0, channel_multiplier=0)
        zero = fixed.tile([P, 1], F32)
        nc.gpsimd.memset(zero[:], 0.0)
        warm = fixed.tile([P, 1], F32)
        nc.scalar.activation(out=warm[:], in_=zero[:], func=ACT.Sin)
        identity = fixed.tile([P, P], F32)
        make_identity(nc, identity[:])
        sines = fixed.tile([P, J, 3, PAIRS], F32)
        table = fixed.tile([P, J, 2, PAIRS, 2], F32)

        x_codes = fixed.tile([P, J, PASSES, P], U32, align_bytes=64)
        x_scales = fixed.tile([P, J, PASSES, P], U8, align_bytes=64)
        w_codes = {}
        w_scales = {}
        grouped_x = {}
        grouped_w = {}

        def flip_block(words, grouped, on_vector, ordered=False):
            bank = bank_pool.tile([P, PASSES, 2, P], F32, name="bank", bufs=4)
            for s in range(PASSES):
                if ordered:
                    for u in range(2):
                        nc.tensor.transpose(bank[:, s, u, :], words[:, s, u, :], identity[:])
                else:
                    transpose_words(nc, bank[:, s], words, identity, s)
            in_ = bank[:].rearrange("p s u r -> p s r u")
            if on_vector:
                nc.vector.tensor_copy(out=grouped.bitcast(F32), in_=in_)
            else:
                nc.scalar.copy(out=grouped.bitcast(F32), in_=in_)

        def flip_x(first, count):
            grouped = grouped_pool.tile(
                [P, count, PASSES, P, PACK], BF16, align_bytes=64, name="grouped_x%d" % count
            )
            for k in range(count):
                flip_block(x_rows[first + k].bitcast(F32), grouped[:, k], False)
            grouped_x[first] = grouped

        def quantise_x(first, count):
            tokens = slice(first, first + count)
            nc.vector.quantize_mx(
                out=x_codes[:, tokens].rearrange("p j s n -> p (j s n)").bitcast(FP8X4),
                scales=x_scales[:, tokens].rearrange("p j s n -> p (j s n)"),
                in_=grouped_x[first][:].rearrange("p j s n t -> p (j s n t)"),
            )

        words_of = {}

        def order_words(t, half):
            words = word_pool.tile([P, 2, PASSES, 2, P], F32, name="words")
            nc.scalar.copy(
                out=words[:].rearrange("p n s u q -> p (n s) u q"),
                in_=w_halves[t, half][:]
                .rearrange("p n c -> p (n c)")
                .bitcast(F32)
                .rearrange("p (m q u) -> p m u q", q=P, u=2),
            )
            words_of[t, half] = words

        def flip_w(t, half, on_vector=(False, False)):
            if half == 0:
                grouped_w[t] = grouped_pool.tile(
                    [P, 2, PASSES, HALF, PACK], BF16, align_bytes=64, name="grouped_w"
                )
                w_codes[t] = w_mx.tile([P, 2, PASSES, HALF], U32, align_bytes=64, name="codes")
                w_scales[t] = w_mx.tile([P, 2, PASSES, HALF], U8, align_bytes=64, name="scales")
            for n in range(2):
                ordered = (t, half) in words_of
                flip_block(
                    words_of[t, half][:, n] if ordered else w_halves[t, half][:, n, :].bitcast(F32),
                    grouped_w[t][:, half, :, n * P : (n + 1) * P, :],
                    on_vector[n],
                    ordered,
                )

        def quantise_w(t, halves=slice(0, 2)):
            nc.vector.quantize_mx(
                out=w_codes[t][:, halves].rearrange("p g s n -> p (g s n)").bitcast(FP8X4),
                scales=w_scales[t][:, halves].rearrange("p g s n -> p (g s n)"),
                in_=grouped_w[t][:, halves].rearrange("p g s n t -> p (g s n t)"),
            )

        products = {}

        def multiply(t, half, pair):
            rotated = tiles[t][0] != VALUE
            product = bank_pool.tile(
                [P, 2, HALF], F32, name="product" if rotated else "bank", bufs=4 if rotated else 4
            )
            for k in range(2):
                for s in range(PASSES):
                    nc.tensor.matmul_mx(
                        out=product[:, k, :],
                        lhsT=x_codes[:, 2 * pair + k, s, :].bitcast(FP8X4),
                        lhsT_scale=x_scales[:, 2 * pair + k, s, :],
                        rhs=w_codes[t][:, half, s, :].bitcast(FP8X4),
                        rhs_scale=w_scales[t][:, half, s, :],
                        start=(s == 0),
                        stop=(s == PASSES - 1),
                    )
            products[t, half, pair] = product

        results = {}

        terms_of = {}

        def result_start(t, half, pair):
            size, pairs = store_group(t, half, pair)
            if pair == pairs.start:
                results[t, half] = result_pool.tile(
                    [P, HEADS, 2 * (pairs.stop - pairs.start), DH], F32, name="result"
                )

        def result_of(t, half, pair, width):
            size, pairs = store_group(t, half, pair)
            last = 2 * (pair - pairs.start) + 2
            return results[t, half][:, :, last - width : last, :].rearrange("p h j d -> p j h d")

        def store_group(t, half, pair):
            size = J // 2
            if t == 0:
                size = 2
            if (t, half) == LAST_HALF:
                size = 2
            return size, slice(pair - pair % size, pair - pair % size + size)

        def finish(t, half, pair):
            size, pairs = store_group(t, half, pair)
            if pair != pairs.stop - 1:
                return
            part, head_half, dest = tiles[t]
            first_head = 2 * HEADS * head_half + HEADS * half
            tokens = slice(2 * pairs.start, 2 * pairs.stop)
            for b in range(B):
                nc.sync.dma_start(
                    out=dest[b, first_head : first_head + HEADS].rearrange("h (g j) d -> g h j d", j=J)[
                        :, :, tokens, :
                    ],
                    in_=results[t, half][b:P:B],
                )

        def rotate(t, half, pair):
            width = 4 if t > 0 else 2
            first = 2 * (pair % 2) if width == 4 else 0
            if first == 0:
                terms_of[0] = terms_pool.tile(
                    [P, width, 2, HEADS, DH], F32, name="terms%d" % width, bufs=3
                )
            terms = terms_of[0]
            shape = [P, 4, HEADS, PAIRS, 2]
            product = products[t, half, pair][:].rearrange("p k (e h i) -> p (k e) h i", e=2, h=HEADS)
            factors = table[:, 2 * pair : 2 * pair + 2].rearrange("p k e i r -> p (k e) i r")
            nc.vector.tensor_tensor(
                out=terms[:, first : first + 2].rearrange("p k e h (i r) -> p (k e) h i r", r=2),
                in0=product.unsqueeze(4).to_broadcast(shape),
                in1=factors.unsqueeze(2).to_broadcast(shape),
                op=ALU.mult,
            )
            result_start(t, half, pair)
            if first + 2 < width:
                return
            adder = nc.vector if (t, half, pair) == steps[-1] else nc.gpsimd
            adder.tensor_tensor(
                out=result_of(t, half, pair, width), in0=terms[:, :, 0], in1=terms[:, :, 1], op=ALU.add
            )
            finish(t, half, pair)

        def copy_value(t, half, pair):
            result_start(t, half, pair)
            nc.scalar.copy(
                out=result_of(t, half, pair, 2),
                in_=products[t, half, pair][:].rearrange("p k (h d) -> p k h d", h=HEADS),
            )
            finish(t, half, pair)

        steps = [(0, half, pair) for pair in range(J // 2) for half in range(2)]
        copies = []
        for t in range(1, len(tiles)):
            for half in range(2):
                for pair in range(J // 2):
                    if tiles[t][0] == VALUE:
                        copies.append((t, half, pair))
                    else:
                        steps.append((t, half, pair))
        LAST_HALF = steps[-1][:2]

        phased = build_angles(nc, fixed, partition, token)
        flip_x(0, 1)
        quantise_x(0, 1)
        flip_w(0, 0, (False, True))
        make_sines(nc, sines, phased, slice(0, 2))
        square_sines(nc, sines, table, slice(0, 2))
        flip_x(1, 1)
        quantise_w(0, slice(0, 1))
        finish_table(nc.vector, table, slice(0, 2))
        quantise_x(1, 1)
        make_sines(nc, sines, phased, slice(2, J))
        flip_w(0, 1, (False, True))
        multiply(*steps[0])
        quantise_w(0, slice(1, 2))
        rotate(*steps[0])
        square_sines(nc, sines, table, slice(2, J))
        flip_x(2, 2)
        multiply(*steps[1])
        quantise_x(2, 2)
        finish_table(nc.vector, table, slice(2, J))
        rotate(*steps[1])
        flip_x(4, 2)
        multiply(*steps[2])
        multiply(*steps[3])
        rotate(*steps[2])
        quantise_x(4, 2)
        flip_x(6, 2)
        flip_w(2, 0)
        flip_w(2, 1)
        multiply(*steps[4])
        multiply(*steps[5])
        rotate(*steps[3])
        quantise_x(6, 2)
        made = 6
        done = 4
        copied = 0
        ready = {0}
        flips = {5: [(1, 0)], 6: [(1, 1)], 8: [(3, 0)], 9: [(3, 1)], 12: [(4, 0)], 13: [(4, 1)], 17: [(5, 0)], 18: [(5, 1)]}
        quants = {4: 2, 9: 1, 11: 3, 15: 4, 21: 5}
        for r in range(done, len(steps)):
            for t, half in flips.get(r, []):
                flip_w(t, half)
            rotate(*steps[r])
            for t, half in flips.get(r + 3, []):
                if t in [4, 5]:
                    order_words(t, half)
            if r in quants:
                quantise_w(quants[r])
                ready.add(quants[r])
            while made < min(r + 1 + 3, len(steps)):
                t, half, pair = steps[made]
                if t not in ready:
                    break
                multiply(t, half, pair)
                made += 1
            want = (r + 1 - 9) * len(copies) // (len(steps) - 9 - 9)
            while copied < min(want, len(copies)) and copies[copied][0] in ready:
                multiply(*copies[copied])
                copy_value(*copies[copied])
                copied += 1
